import numpy as np
import ml_dtypes


def mxq(x, axis, fmt="e4m3"):
    dtype, down = {"e4m3": (ml_dtypes.float8_e4m3fn, 7), "e5m2": (ml_dtypes.float8_e5m2, 14)}[fmt]
    v = np.moveaxis(np.asarray(x, np.float32).astype(ml_dtypes.bfloat16).astype(np.float64), axis, -1)
    blocks = v.reshape(v.shape[:-1] + (-1, 32))
    amax = np.abs(blocks).max(-1, keepdims=True)
    byte = np.maximum(np.where(amax > 0, np.frexp(amax)[1] - 1 + 127, 0) - down, 1)
    scale = np.exp2(byte - 127.0)
    codes = (blocks / scale).astype(np.float32).astype(dtype).astype(np.float64)
    return np.moveaxis((codes * scale).reshape(v.shape), -1, axis)


WIDE = False


def mx_kscale(k):
    if not WIDE:
        return np.ones(k)
    levels = np.array([10, -10, 5, -5, 0])
    a = np.random.permutation(np.resize(levels, k // 512 * 4)).reshape(k // 512, 4)
    idx = np.arange(k)
    return np.exp2(a[idx // 512, idx % 128 // 32])


BF16 = ml_dtypes.bfloat16


def bf(x):
    return np.asarray(x, np.float32).astype(BF16)


def f64(x):
    return np.asarray(x).astype(np.float64)


B, C, H, W, K, O = 4, 256, 32, 32, 2, 1024
P = C * K * K
PAD = 1
G = 32


def im2col(a):
    a_pad = np.pad(a, ((0, 0), (0, 0), (PAD, PAD), (PAD, PAD)), mode="reflect")
    cols = np.stack([a_pad[:, :, kh:kh + H, kw:kw + W] for kh in range(K) for kw in range(K)], axis=2)
    cols = cols.reshape(B, P, H * W)
    return np.swapaxes(cols, 1, 2)


def setup_inputs():
    u = np.unique(mx_kscale(P))
    t = u[np.arange(C // G) % len(u)]
    sc = np.repeat(t, G).reshape(1, C, 1, 1)
    sp = np.repeat(t, G * K * K).reshape(P, 1)
    lam = 1.0 if len(u) == 1 else 0.0
    g = 2.0 ** np.round(0.5 * np.log2(np.mean(t ** 2)))
    amp = 0.5 + 1.5 * np.random.random_sample((B, 1, H, W))
    off = 0.6 + 0.4 * np.random.standard_normal((B, 1, H, W))
    bound = np.sqrt(6.0 / P)
    z = np.random.standard_normal((B, C, H, W))
    z[:, 1::2] = lam * z[:, 1::2] - (1.0 - lam) * z[:, 0::2]
    return {"a": bf((z * amp + off * lam) * sc),
            "conv_kernel": bf(np.random.uniform(-bound, bound, (P, O)) * g / sp)}


def reference(a, conv_kernel):
    patches = im2col(f64(a))
    mean = np.mean(patches, axis=-1, keepdims=True)
    std = np.std(patches, axis=-1, keepdims=True, ddof=1)
    normed = (patches - mean) / std
    out = mxq(normed, 2, "e4m3") @ mxq(f64(conv_kernel), 0, "e4m3")
    return np.swapaxes(out, 1, 2).reshape(B, O, H, W)

@@ -1,0 +1,289 @@
+from contextlib import ExitStack
+
+import concourse.mybir as mybir
+from concourse.masks import make_identity
+
+FLOPS = 2 * 4096 * 1024 * 1024
+
+BF16 = mybir.dt.bfloat16
+F32 = mybir.dt.float32
+U32 = mybir.dt.uint32
+U8 = mybir.dt.uint8
+FP8X4 = mybir.dt.float8_e4m3fn_x4
+ALU = mybir.AluOpType
+ACT = mybir.ActivationFunctionType
+
+P = 128
+NB = 4
+TPI = 8
+Z_IN = 130
+
+
+def tile_norm_conv_t_kernel(tc, a, conv_kernel, out):
+    nc = tc.nc
+    with ExitStack() as ctx:
+        const = ctx.enter_context(tc.tile_pool(name="const", bufs=1))
+        keep = ctx.enter_context(tc.tile_pool(name="keep", bufs=1))
+        small = ctx.enter_context(tc.tile_pool(name="small", bufs=2))
+        npool = ctx.enter_context(tc.tile_pool(name="npool", bufs=4))
+        gpool = ctx.enter_context(tc.tile_pool(name="gpool", bufs=2))
+        opool = ctx.enter_context(tc.tile_pool(name="opool", bufs=6))
+        ps_f = ctx.enter_context(tc.psum_pool(name="ps_f", bufs=2))
+        ps_b = ctx.enter_context(tc.psum_pool(name="ps_b", bufs=3))
+        ps_o = ctx.enter_context(tc.psum_pool(name="ps_o", bufs=3))
+
+        a_sb = []
+        for b in range(NB):
+            a_b = keep.tile([P, 2, 1024], BF16, name="a_sb%d" % b)
+            a_sb.append(a_b)
+        w_raw = keep.tile([P, 2, 4, 1024], BF16, name="w_raw")
+        w_view = conv_kernel.rearrange("(q e k w) o -> q k e (w o)", e=2, k=2, w=2)
+
+        def load_a(b):
+            nc.sync.dma_start(
+                out=a_sb[b][:],
+                in_=a[b].rearrange("(h c) i j -> c h (i j)", h=2),
+            )
+
+        load_a(0)
+        for kh in range(2):
+            nc.sync.dma_start(out=w_raw[:, kh].rearrange("q (e w) o -> q e (w o)", e=2), in_=w_view[:, kh])
+        for b in range(1, NB):
+            load_a(b)
+
+        one = const.tile([P, 1], F32, name="one")
+        nc.vector.memset(one[:], 1.0)
+        one_rt = const.tile([P, 1], F32, name="one_rt")
+        nc.scalar.activation(out=one_rt[:], in_=one[:], func=ACT.Sqrt)
+
+        identb = const.tile([P, P], BF16, name="identb")
+        make_identity(nc, identb[:])
+        shiftb = const.tile([P, P], BF16, name="shiftb")
+        nc.vector.memset(shiftb[:], 0.0)
+        nc.vector.tensor_copy(out=shiftb[:, 1:P], in_=identb[:, 0 : P - 1])
+        identf = const.tile([P, P], F32, name="identf")
+        make_identity(nc, identf[:])
+
+        diag = const.tile([P, 388], F32, name="diag")
+        nc.gpsimd.memset(diag[:], 0.0)
+        nc.vector.tensor_copy(out=diag[:, Z_IN : Z_IN + P], in_=identf[:])
+        pair = const.tile([P, 388], F32, name="pair")
+        nc.vector.tensor_tensor(out=pair[:, 0:387], in0=diag[:, 0:387], in1=diag[:, 1:388], op=ALU.add)
+        band = const.tile([P, 356], F32, name="band")
+        nc.vector.tensor_tensor(out=band[:, 0:355], in0=pair[:, 0:355], in1=pair[:, 32:387], op=ALU.add)
+        band_odd = const.tile([P, 356], F32, name="band_odd")
+        nc.vector.tensor_copy(
+            out=band_odd[:, 0:354].rearrange("p (k t) -> p k t", t=2),
+            in_=band[:, 0:354].rearrange("p (k t) -> p k t", t=2)[:, :, 0:1].to_broadcast([P, 177, 2]),
+        )
+        band_even = const.tile([P, 356], F32, name="band_even")
+        nc.vector.tensor_copy(
+            out=band_even[:, 1:355].rearrange("p (k t) -> p k t", t=2),
+            in_=band[:, 1:355].rearrange("p (k t) -> p k t", t=2)[:, :, 0:1].to_broadcast([P, 177, 2]),
+        )
+        bands = [band_even, band_odd]
+
+        wg = keep.tile([P, 2, 1024, 4], BF16, name="wg", align_bytes=64)
+        wc = keep.tile([P, 2, 1024], U32, name="wc", align_bytes=64)
+        ws = keep.tile([P, 2, 1024], U8, name="ws", align_bytes=64)
+
+        def prep_weights():
+            for half in range(2):
+                cols = slice(512 * half, 512 * half + 512)
+                for kh in range(2):
+                    dst = wg[:, kh, cols, :].rearrange("q (c i) t -> q c t i", i=4)
+                    src = w_raw[:, kh, :, cols].rearrange("q t (c i) -> q c t i", i=4)
+                    if half == 0:
+                        nc.vector.tensor_copy(out=dst, in_=src)
+                    else:
+                        nc.scalar.copy(out=dst, in_=src)
+            for half in range(2):
+                cols = slice(512 * half, 512 * half + 512)
+                for kh in range(2):
+                    nc.vector.quantize_mx(
+                        out=wc[:, kh, cols].bitcast(FP8X4),
+                        scales=ws[:, kh, cols],
+                        in_=wg[:, kh, cols].rearrange("q o t -> q (o t)"),
+                    )
+
+        a_t = []
+        means = []
+        rstds = []
+
+        def stage_a(b):
+            a_tb = keep.tile([P, TPI, 256], BF16, name="a_t%d" % b)
+            a_t.append(a_tb)
+            sums = keep.tile([P, 2, 16], F32, name="sums%d" % b)
+            nc.vector.memset(sums[:], 0.0)
+            for quad in range(2):
+                f_t = ps_f.tile([P, 4, 256], BF16, name="f_t", tag="front")
+                for tl in range(4):
+                    t = 4 * quad + tl
+                    for e in range(2):
+                        nc.tensor.transpose(
+                            out=f_t[:, tl, P * e : P * e + P],
+                            in_=a_sb[b][:, e, P * t : P * t + P],
+                            identity=identb[:],
+                        )
+                for tl in range(4):
+                    t = 4 * quad + tl
+                    nc.vector.tensor_scalar(
+                        out=a_tb[:, t, :],
+                        in0=f_t[:, tl, :],
+                        scalar1=1.0,
+                        scalar2=None,
+                        op0=ALU.mult,
+                        op1=ALU.add,
+                        accum_out=sums[:, 0, t + 1 : t + 2],
+                    )
+                    junk = small.tile([P, 256], BF16, name="junk")
+                    nc.scalar.activation(
+                        out=junk[:], in_=a_tb[:, t, :], func=ACT.Square, accum_out=sums[:, 1, t + 1 : t + 2]
+                    )
+            win = ps_f.tile([P, 4, 2, TPI], F32, name="win", tag="front")
+            for kh in range(2):
+                side = 1 if kh == 0 else -1
+                for phi in range(2):
+                    v = 2 * kh + phi
+                    z0 = Z_IN - 32 * kh
+                    nc.tensor.matmul(
+                        out=win[:, v],
+                        lhsT=bands[phi][:, z0 : z0 + P],
+                        rhs=sums[:, :, 1 : 1 + TPI],
+                        start=True,
+                        stop=False,
+                    )
+                    z1 = z0 - P * side
+                    nc.tensor.matmul(
+                        out=win[:, v],
+                        lhsT=bands[phi][:, z1 : z1 + P],
+                        rhs=sums[:, :, 1 + side : 1 + side + TPI],
+                        start=False,
+                        stop=True,
+                    )
+            mean = keep.tile([P, 4, TPI], F32, name="mean%d" % b)
+            nc.vector.tensor_scalar(
+                out=mean[:], in0=win[:, :, 0, :], scalar1=1.0 / 1024.0, scalar2=None, op0=ALU.mult
+            )
+            sq = small.tile([P, 4, TPI], F32, name="sq")
+            nc.vector.tensor_tensor(out=sq[:], in0=mean[:], in1=win[:, :, 0, :], op=ALU.mult)
+            dev = small.tile([P, 4, TPI], F32, name="dev")
+            nc.vector.tensor_tensor(out=dev[:], in0=win[:, :, 1, :], in1=sq[:], op=ALU.subtract)
+            std = small.tile([P, 4, TPI], F32, name="std")
+            nc.scalar.activation(out=std[:], in_=dev[:], func=ACT.Sqrt, scale=1.0 / 1023.0)
+            rstd = keep.tile([P, 4, TPI], F32, name="rstd%d" % b)
+            nc.vector.reciprocal(out=rstd[:], in_=std[:])
+            means.append(mean)
+            rstds.append(rstd)
+
+        grouped = {}
+        codes = {}
+        scales = {}
+
+        def stage_b_open(b):
+            grouped[b] = gpool.tile([P, 2, 2, 32, 16, 4], BF16, name="grouped", align_bytes=64)
+            codes[b] = gpool.tile([P, 2, 2, 2, 256], U32, name="codes", align_bytes=64)
+            scales[b] = gpool.tile([P, 2, 2, 2, 256], U8, name="scales", align_bytes=64)
+
+        def stage_b_bank(b, quad, kh, phi, on_vector):
+            v = 2 * kh + phi
+            g = grouped[b]
+            n_q = npool.tile([P, 4, 256], BF16, name="n_q")
+            for tl in range(4):
+                t = 4 * quad + tl
+                nc.vector.tensor_scalar(
+                    out=n_q[:, tl, :],
+                    in0=a_t[b][:, t, :],
+                    scalar1=means[b][:, v, t : t + 1],
+                    scalar2=rstds[b][:, v, t : t + 1],
+                    op0=ALU.subtract,
+                    op1=ALU.mult,
+                )
+            bk = ps_b.tile([P, 2, 512], BF16, name="bk")
+            perm = identb if phi == 1 else shiftb
+            for tl in range(4):
+                for e in range(2):
+                    nc.tensor.transpose(
+                        out=bk[:, e, P * tl : P * tl + P],
+                        in_=n_q[:, tl, e:256:2],
+                        identity=perm[:],
+                    )
+            lo = 1 if (kh == 1 and quad == 0) else 0
+            hi = 15 if (kh == 0 and quad == 1) else 16
+            r0 = 16 * quad + lo + 1 - kh
+            r1 = 16 * quad + hi + 1 - kh
+            dst = g[:, kh, phi, r0:r1].rearrange("p i j (e k) -> p (i j) e k", e=2)
+            src = bk[:, :, 32 * lo : 32 * hi].rearrange("p e (x k) -> p x e k", k=2)
+            if on_vector:
+                nc.vector.tensor_copy(out=dst, in_=src)
+            else:
+                nc.scalar.copy(out=dst, in_=src)
+
+        def stage_b_close(b, quad):
+            g = grouped[b]
+            r0 = 1 if quad == 0 else 16
+            r1 = 16 * quad + 16
+            for kw in range(2):
+                nc.gpsimd.tensor_copy(
+                    out=g[:, :, 0, r0:r1, 0, kw:4:2], in_=g[:, :, 1, r0:r1, 0, 1 - kw : 4 : 2]
+                )
+            if quad == 0:
+                for kh in range(2):
+                    nc.gpsimd.tensor_copy(out=g[:, kh, :, 0], in_=g[:, 1 - kh, :, 1])
+            for kh in range(2):
+                for phi in range(2):
+                    nc.vector.quantize_mx(
+                        out=codes[b][:, kh, quad, phi, :].bitcast(FP8X4),
+                        scales=scales[b][:, kh, quad, phi, :],
+                        in_=g[:, kh, phi, 16 * quad : 16 * quad + 16].rearrange("p i j t -> p (i j t)"),
+                    )
+
+        def stage_c(b, quad, m):
+            acc = ps_o.tile([P, 512], F32, name="acc")
+            for kh in range(2):
+                nc.tensor.matmul_mx(
+                    out=acc[:],
+                    lhsT=wc[:, kh, P * m : P * m + P].bitcast(FP8X4),
+                    lhsT_scale=ws[:, kh, P * m : P * m + P],
+                    rhs=codes[b][:, kh, quad].rearrange("p f x -> p (f x)").bitcast(FP8X4),
+                    rhs_scale=scales[b][:, kh, quad].rearrange("p f x -> p (f x)"),
+                    start=(kh == 0),
+                    stop=(kh == 1),
+                )
+            o_sb = opool.tile([P, 512], F32, name="o_sb")
+            dst = o_sb[:].rearrange("p (x f) -> p x f", f=2)
+            src = acc[:].rearrange("p (f x) -> p x f", f=2)
+            if m % 2 == 0:
+                nc.vector.tensor_copy(out=dst, in_=src)
+            else:
+                nc.scalar.copy(out=dst, in_=src)
+            nc.sync.dma_start(
+                out=out[b, P * m : P * m + P, 16 * quad : 16 * quad + 16, :].rearrange("o i j -> o (i j)"),
+                in_=o_sb[:],
+            )
+
+        variants = [(kh, phi) for kh in range(2) for phi in range(2)]
+
+        stage_a(0)
+        prep_weights()
+        stage_b_open(0)
+        for i, (kh, phi) in enumerate(variants):
+            stage_b_bank(0, 0, kh, phi, i % 2 == 0)
+        stage_b_close(0, 0)
+        for n in range(2 * NB):
+            b, quad = n // 2, n % 2
+            nb, nquad = (n + 1) // 2, (n + 1) % 2
+            more = n + 1 < 2 * NB
+            if quad == 0 and b + 1 < NB:
+                stage_a(b + 1)
+            if more and nquad == 0:
+                stage_b_open(nb)
+            for part in range(2):
+                if more:
+                    for i in (2 * part, 2 * part + 1):
+                        kh, phi = variants[i]
+                        stage_b_bank(nb, nquad, kh, phi, i == 0)
+                    if part == 1:
+                        stage_b_close(nb, nquad)
+                for m in range(4 * part, 4 * part + 4):
+                    stage_c(b, quad, m)

@@ -16,7 +16,9 @@ ACT = mybir.ActivationFunctionType
 P = 128
 NB = 4
 TPI = 8
+NCH = 2 * NB
 Z_IN = 130
+VARIANTS = [(0, 0), (0, 1), (1, 0), (1, 1)]
 
 
 def tile_norm_conv_t_kernel(tc, a, conv_kernel, out):
@@ -25,31 +27,35 @@ def tile_norm_conv_t_kernel(tc, a, conv_kernel, out):
         const = ctx.enter_context(tc.tile_pool(name="const", bufs=1))
         keep = ctx.enter_context(tc.tile_pool(name="keep", bufs=1))
         small = ctx.enter_context(tc.tile_pool(name="small", bufs=2))
-        npool = ctx.enter_context(tc.tile_pool(name="npool", bufs=4))
+        npool = ctx.enter_context(tc.tile_pool(name="npool", bufs=8))
         gpool = ctx.enter_context(tc.tile_pool(name="gpool", bufs=2))
         opool = ctx.enter_context(tc.tile_pool(name="opool", bufs=6))
-        ps_f = ctx.enter_context(tc.psum_pool(name="ps_f", bufs=2))
-        ps_b = ctx.enter_context(tc.psum_pool(name="ps_b", bufs=3))
+        ps_w = ctx.enter_context(tc.psum_pool(name="ps_w", bufs=5))
         ps_o = ctx.enter_context(tc.psum_pool(name="ps_o", bufs=3))
+        ctx.enter_context(tc.manual_schedule())
 
         a_sb = []
         for b in range(NB):
             a_b = keep.tile([P, 2, 1024], BF16, name="a_sb%d" % b)
             a_sb.append(a_b)
         w_raw = keep.tile([P, 2, 4, 1024], BF16, name="w_raw")
-        w_view = conv_kernel.rearrange("(q e k w) o -> q k e (w o)", e=2, k=2, w=2)
+        w_view = conv_kernel.rearrange("(q e k w) o -> q e k w o", e=2, k=2, w=2)
 
         def load_a(b):
-            nc.sync.dma_start(
-                out=a_sb[b][:],
-                in_=a[b].rearrange("(h c) i j -> c h (i j)", h=2),
-            )
+            nc.sync.dma_start(out=a_sb[b][:], in_=a[b].rearrange("(h c) i j -> c h (i j)", h=2))
+
+        def load_w(half):
+            cols = slice(512 * half, 512 * half + 512)
+            for kh in range(2):
+                for e in range(2):
+                    nc.sync.dma_start(out=w_raw[:, kh, 2 * e : 2 * e + 2, cols], in_=w_view[:, e, kh, :, cols])
 
         load_a(0)
-        for kh in range(2):
-            nc.sync.dma_start(out=w_raw[:, kh].rearrange("q (e w) o -> q e (w o)", e=2), in_=w_view[:, kh])
-        for b in range(1, NB):
-            load_a(b)
+        load_a(1)
+        load_w(0)
+        load_w(1)
+        load_a(2)
+        load_a(3)
 
         one = const.tile([P, 1], F32, name="one")
         nc.vector.memset(one[:], 1.0)
@@ -58,14 +64,13 @@ def tile_norm_conv_t_kernel(tc, a, conv_kernel, out):
 
         identb = const.tile([P, P], BF16, name="identb")
         make_identity(nc, identb[:])
+        identf = const.tile([P, P], F32, name="identf")
+        make_identity(nc, identf[:])
+        diag = const.tile([P, 388], F32, name="diag")
+        nc.gpsimd.memset(diag[:], 0.0)
         shiftb = const.tile([P, P], BF16, name="shiftb")
         nc.vector.memset(shiftb[:], 0.0)
         nc.vector.tensor_copy(out=shiftb[:, 1:P], in_=identb[:, 0 : P - 1])
-        identf = const.tile([P, P], F32, name="identf")
-        make_identity(nc, identf[:])
-
-        diag = const.tile([P, 388], F32, name="diag")
-        nc.gpsimd.memset(diag[:], 0.0)
         nc.vector.tensor_copy(out=diag[:, Z_IN : Z_IN + P], in_=identf[:])
         pair = const.tile([P, 388], F32, name="pair")
         nc.vector.tensor_tensor(out=pair[:, 0:387], in0=diag[:, 0:387], in1=diag[:, 1:388], op=ALU.add)
@@ -81,164 +86,190 @@ def tile_norm_conv_t_kernel(tc, a, conv_kernel, out):
             out=band_even[:, 1:355].rearrange("p (k t) -> p k t", t=2),
             in_=band[:, 1:355].rearrange("p (k t) -> p k t", t=2)[:, :, 0:1].to_broadcast([P, 177, 2]),
         )
+        nc.vector.tensor_copy(out=band_even[:, 2:354:32], in_=band[:, 2:354:32])
         bands = [band_even, band_odd]
 
         wg = keep.tile([P, 2, 1024, 4], BF16, name="wg", align_bytes=64)
         wc = keep.tile([P, 2, 1024], U32, name="wc", align_bytes=64)
         ws = keep.tile([P, 2, 1024], U8, name="ws", align_bytes=64)
 
-        def prep_weights():
-            for half in range(2):
-                cols = slice(512 * half, 512 * half + 512)
-                for kh in range(2):
-                    dst = wg[:, kh, cols, :].rearrange("q (c i) t -> q c t i", i=4)
-                    src = w_raw[:, kh, :, cols].rearrange("q t (c i) -> q c t i", i=4)
-                    if half == 0:
-                        nc.vector.tensor_copy(out=dst, in_=src)
-                    else:
-                        nc.scalar.copy(out=dst, in_=src)
-            for half in range(2):
-                cols = slice(512 * half, 512 * half + 512)
-                for kh in range(2):
-                    nc.vector.quantize_mx(
-                        out=wc[:, kh, cols].bitcast(FP8X4),
-                        scales=ws[:, kh, cols],
-                        in_=wg[:, kh, cols].rearrange("q o t -> q (o t)"),
+        def regroup_w(half, kh, engine):
+            cols = slice(512 * half, 512 * half + 512)
+            dst = wg[:, kh, cols, :].rearrange("q (c i) t -> q c t i", i=4)
+            src = w_raw[:, kh, :, cols].rearrange("q t (c i) -> q c t i", i=4)
+            if engine == "v":
+                nc.vector.tensor_copy(out=dst, in_=src)
+            elif engine == "s":
+                nc.scalar.copy(out=dst, in_=src)
+            else:
+                nc.gpsimd.tensor_scalar(out=dst, in0=src, scalar1=1.0, scalar2=0.0, op0=ALU.mult, op1=ALU.add)
+
+        def quantise_w(half, kh):
+            cols = slice(512 * half, 512 * half + 512)
+            nc.vector.quantize_mx(
+                out=wc[:, kh, cols].bitcast(FP8X4),
+                scales=ws[:, kh, cols],
+                in_=wg[:, kh, cols].rearrange("q o t -> q (o t)"),
+            )
+
+        a_t = {}
+        sums = {}
+        front = {}
+        wins = {}
+        means = {}
+        rstds = {}
+        devs = {}
+        stds = {}
+
+        def fwd(b, quad):
+            if quad == 0:
+                a_t[b] = keep.tile([P, TPI, 256], BF16, name="a_t%d" % b)
+                sums[b] = keep.tile([P, 2, 16], F32, name="sums%d" % b)
+                nc.vector.memset(sums[b][:], 0.0)
+            f_t = ps_w.tile([P, 4, 256], BF16, name="f_t", tag="work")
+            front[(b, quad)] = f_t
+            for tl in range(4):
+                t = 4 * quad + tl
+                for h in range(2):
+                    nc.tensor.transpose(
+                        out=f_t[:, tl, P * h : P * h + P],
+                        in_=a_sb[b][:, h, P * t : P * t + P],
+                        identity=identb[:],
                     )
 
-        a_t = []
-        means = []
-        rstds = []
+        def evac(b, quad):
+            for tl in range(4):
+                t = 4 * quad + tl
+                nc.vector.tensor_scalar(
+                    out=a_t[b][:, t, :],
+                    in0=front[(b, quad)][:, tl, :],
+                    scalar1=1.0,
+                    scalar2=None,
+                    op0=ALU.mult,
+                    op1=ALU.add,
+                    accum_out=sums[b][:, 0, t + 1 : t + 2],
+                )
 
-        def stage_a(b):
-            a_tb = keep.tile([P, TPI, 256], BF16, name="a_t%d" % b)
-            a_t.append(a_tb)
-            sums = keep.tile([P, 2, 16], F32, name="sums%d" % b)
-            nc.vector.memset(sums[:], 0.0)
-            for quad in range(2):
-                f_t = ps_f.tile([P, 4, 256], BF16, name="f_t", tag="front")
-                for tl in range(4):
-                    t = 4 * quad + tl
-                    for e in range(2):
-                        nc.tensor.transpose(
-                            out=f_t[:, tl, P * e : P * e + P],
-                            in_=a_sb[b][:, e, P * t : P * t + P],
-                            identity=identb[:],
-                        )
-                for tl in range(4):
-                    t = 4 * quad + tl
-                    nc.vector.tensor_scalar(
-                        out=a_tb[:, t, :],
-                        in0=f_t[:, tl, :],
-                        scalar1=1.0,
-                        scalar2=None,
-                        op0=ALU.mult,
-                        op1=ALU.add,
-                        accum_out=sums[:, 0, t + 1 : t + 2],
-                    )
-                    junk = small.tile([P, 256], BF16, name="junk")
-                    nc.scalar.activation(
-                        out=junk[:], in_=a_tb[:, t, :], func=ACT.Square, accum_out=sums[:, 1, t + 1 : t + 2]
-                    )
-            win = ps_f.tile([P, 4, 2, TPI], F32, name="win", tag="front")
-            for kh in range(2):
+        def squares(b, quad):
+            for tl in range(4):
+                t = 4 * quad + tl
+                junk = small.tile([P, 256], BF16, name="junk")
+                nc.scalar.activation(
+                    out=junk[:], in_=a_t[b][:, t, :], func=ACT.Square, accum_out=sums[b][:, 1, t + 1 : t + 2]
+                )
+
+        def window_sums(b):
+            win = ps_w.tile([P, 4, 2, TPI], F32, name="win", tag="work")
+            wins[b] = win
+            for v, (kh, phi) in enumerate(VARIANTS):
                 side = 1 if kh == 0 else -1
-                for phi in range(2):
-                    v = 2 * kh + phi
-                    z0 = Z_IN - 32 * kh
-                    nc.tensor.matmul(
-                        out=win[:, v],
-                        lhsT=bands[phi][:, z0 : z0 + P],
-                        rhs=sums[:, :, 1 : 1 + TPI],
-                        start=True,
-                        stop=False,
-                    )
-                    z1 = z0 - P * side
-                    nc.tensor.matmul(
-                        out=win[:, v],
-                        lhsT=bands[phi][:, z1 : z1 + P],
-                        rhs=sums[:, :, 1 + side : 1 + side + TPI],
-                        start=False,
-                        stop=True,
-                    )
-            mean = keep.tile([P, 4, TPI], F32, name="mean%d" % b)
+                z0 = Z_IN - 32 * kh
+                nc.tensor.matmul(
+                    out=win[:, v],
+                    lhsT=bands[phi][:, z0 : z0 + P],
+                    rhs=sums[b][:, :, 1 : 1 + TPI],
+                    start=True,
+                    stop=False,
+                )
+                z1 = z0 - P * side
+                nc.tensor.matmul(
+                    out=win[:, v],
+                    lhsT=bands[phi][:, z1 : z1 + P],
+                    rhs=sums[b][:, :, 1 + side : 1 + side + TPI],
+                    start=False,
+                    stop=True,
+                )
+
+        def math_1(b):
+            win = wins[b]
+            means[b] = keep.tile([P, 4, TPI], F32, name="mean%d" % b)
             nc.vector.tensor_scalar(
-                out=mean[:], in0=win[:, :, 0, :], scalar1=1.0 / 1024.0, scalar2=None, op0=ALU.mult
+                out=means[b][:], in0=win[:, :, 0, :], scalar1=1.0 / 1024.0, scalar2=None, op0=ALU.mult
             )
             sq = small.tile([P, 4, TPI], F32, name="sq")
-            nc.vector.tensor_tensor(out=sq[:], in0=mean[:], in1=win[:, :, 0, :], op=ALU.mult)
-            dev = small.tile([P, 4, TPI], F32, name="dev")
-            nc.vector.tensor_tensor(out=dev[:], in0=win[:, :, 1, :], in1=sq[:], op=ALU.subtract)
-            std = small.tile([P, 4, TPI], F32, name="std")
-            nc.scalar.activation(out=std[:], in_=dev[:], func=ACT.Sqrt, scale=1.0 / 1023.0)
-            rstd = keep.tile([P, 4, TPI], F32, name="rstd%d" % b)
-            nc.vector.reciprocal(out=rstd[:], in_=std[:])
-            means.append(mean)
-            rstds.append(rstd)
+            nc.vector.tensor_tensor(out=sq[:], in0=means[b][:], in1=win[:, :, 0, :], op=ALU.mult)
+            devs[b] = small.tile([P, 4, TPI], F32, name="dev")
+            nc.vector.tensor_tensor(out=devs[b][:], in0=win[:, :, 1, :], in1=sq[:], op=ALU.subtract)
+
+        def math_root(b):
+            stds[b] = small.tile([P, 4, TPI], F32, name="std")
+            nc.scalar.activation(out=stds[b][:], in_=devs[b][:], func=ACT.Sqrt, scale=1.0 / 1023.0)
+
+        def math_2(b):
+            rstds[b] = keep.tile([P, 4, TPI], F32, name="rstd%d" % b)
+            nc.vector.reciprocal(out=rstds[b][:], in_=stds[b][:])
 
         grouped = {}
         codes = {}
         scales = {}
+        normed = {}
+        back = {}
 
-        def stage_b_open(b):
-            grouped[b] = gpool.tile([P, 2, 2, 32, 16, 4], BF16, name="grouped", align_bytes=64)
-            codes[b] = gpool.tile([P, 2, 2, 2, 256], U32, name="codes", align_bytes=64)
-            scales[b] = gpool.tile([P, 2, 2, 2, 256], U8, name="scales", align_bytes=64)
+        def norm(k):
+            b, quad = k // 2, k % 2
+            for v in range(4):
+                n_q = npool.tile([P, 4, 256], BF16, name="n_q")
+                normed[(k, v)] = n_q
+                for tl in range(4):
+                    t = 4 * quad + tl
+                    nc.vector.tensor_scalar(
+                        out=n_q[:, tl, :],
+                        in0=a_t[b][:, t, :],
+                        scalar1=means[b][:, v, t : t + 1],
+                        scalar2=rstds[b][:, v, t : t + 1],
+                        op0=ALU.subtract,
+                        op1=ALU.mult,
+                    )
 
-        def stage_b_bank(b, quad, kh, phi, on_vector):
-            v = 2 * kh + phi
-            g = grouped[b]
-            n_q = npool.tile([P, 4, 256], BF16, name="n_q")
-            for tl in range(4):
-                t = 4 * quad + tl
-                nc.vector.tensor_scalar(
-                    out=n_q[:, tl, :],
-                    in0=a_t[b][:, t, :],
-                    scalar1=means[b][:, v, t : t + 1],
-                    scalar2=rstds[b][:, v, t : t + 1],
-                    op0=ALU.subtract,
-                    op1=ALU.mult,
-                )
-            bk = ps_b.tile([P, 2, 512], BF16, name="bk")
+        def bwd(k, v):
+            phi = VARIANTS[v][1]
+            bk = ps_w.tile([P, 2, 512], BF16, name="bk", tag="work")
+            back[(k, v)] = bk
             perm = identb if phi == 1 else shiftb
             for tl in range(4):
                 for e in range(2):
                     nc.tensor.transpose(
                         out=bk[:, e, P * tl : P * tl + P],
-                        in_=n_q[:, tl, e:256:2],
+                        in_=normed[(k, v)][:, tl, e:256:2],
                         identity=perm[:],
                     )
+
+        def copy_out(k, v):
+            b, quad = k // 2, k % 2
+            kh, phi = VARIANTS[v]
+            if quad == 0 and v == 0:
+                grouped[b] = gpool.tile([P, 2, 2, 32, 16, 4], BF16, name="grouped", align_bytes=64)
             lo = 1 if (kh == 1 and quad == 0) else 0
             hi = 15 if (kh == 0 and quad == 1) else 16
             r0 = 16 * quad + lo + 1 - kh
             r1 = 16 * quad + hi + 1 - kh
-            dst = g[:, kh, phi, r0:r1].rearrange("p i j (e k) -> p (i j) e k", e=2)
-            src = bk[:, :, 32 * lo : 32 * hi].rearrange("p e (x k) -> p x e k", k=2)
-            if on_vector:
-                nc.vector.tensor_copy(out=dst, in_=src)
-            else:
-                nc.scalar.copy(out=dst, in_=src)
+            nc.vector.tensor_copy(
+                out=grouped[b][:, kh, phi, r0:r1].rearrange("p i j (e k) -> p (i j) e k", e=2),
+                in_=back[(k, v)][:, :, 32 * lo : 32 * hi].rearrange("p e (x k) -> p x e k", k=2),
+            )
 
-        def stage_b_close(b, quad):
+        def fix_quantise(k):
+            b, quad = k // 2, k % 2
             g = grouped[b]
+            if quad == 0:
+                codes[b] = gpool.tile([P, 2, 2, 2, 256], U32, name="codes", align_bytes=64)
+                scales[b] = gpool.tile([P, 2, 2, 2, 256], U8, name="scales", align_bytes=64)
             r0 = 1 if quad == 0 else 16
             r1 = 16 * quad + 16
-            for kw in range(2):
-                nc.gpsimd.tensor_copy(
-                    out=g[:, :, 0, r0:r1, 0, kw:4:2], in_=g[:, :, 1, r0:r1, 0, 1 - kw : 4 : 2]
-                )
+            nc.vector.tensor_copy(out=g[:, :, 0, r0:r1, 0, 0:4:2], in_=g[:, :, 1, r0:r1, 0, 1:4:2])
             if quad == 0:
                 for kh in range(2):
-                    nc.gpsimd.tensor_copy(out=g[:, kh, :, 0], in_=g[:, 1 - kh, :, 1])
-            for kh in range(2):
-                for phi in range(2):
+                    nc.vector.tensor_copy(out=g[:, kh, :, 0], in_=g[:, 1 - kh, :, 1])
+            for phi in (1, 0):
+                for kh in range(2):
                     nc.vector.quantize_mx(
                         out=codes[b][:, kh, quad, phi, :].bitcast(FP8X4),
                         scales=scales[b][:, kh, quad, phi, :],
                         in_=g[:, kh, phi, 16 * quad : 16 * quad + 16].rearrange("p i j t -> p (i j t)"),
                     )
 
-        def stage_c(b, quad, m):
+        def multiply(k, m):
+            b, quad = k // 2, k % 2
             acc = ps_o.tile([P, 512], F32, name="acc")
             for kh in range(2):
                 nc.tensor.matmul_mx(
@@ -251,39 +282,72 @@ def tile_norm_conv_t_kernel(tc, a, conv_kernel, out):
                     stop=(kh == 1),
                 )
             o_sb = opool.tile([P, 512], F32, name="o_sb")
-            dst = o_sb[:].rearrange("p (x f) -> p x f", f=2)
-            src = acc[:].rearrange("p (f x) -> p x f", f=2)
-            if m % 2 == 0:
-                nc.vector.tensor_copy(out=dst, in_=src)
-            else:
-                nc.scalar.copy(out=dst, in_=src)
+            nc.scalar.copy(
+                out=o_sb[:].rearrange("p (x f) -> p x f", f=2), in_=acc[:].rearrange("p (f x) -> p x f", f=2)
+            )
             nc.sync.dma_start(
                 out=out[b, P * m : P * m + P, 16 * quad : 16 * quad + 16, :].rearrange("o i j -> o (i j)"),
                 in_=o_sb[:],
             )
 
-        variants = [(kh, phi) for kh in range(2) for phi in range(2)]
+        def back_to_channels(k):
+            for v in range(4):
+                bwd(k, v)
+                copy_out(k, v)
 
-        stage_a(0)
-        prep_weights()
-        stage_b_open(0)
-        for i, (kh, phi) in enumerate(variants):
-            stage_b_bank(0, 0, kh, phi, i % 2 == 0)
-        stage_b_close(0, 0)
-        for n in range(2 * NB):
-            b, quad = n // 2, n % 2
-            nb, nquad = (n + 1) // 2, (n + 1) % 2
-            more = n + 1 < 2 * NB
-            if quad == 0 and b + 1 < NB:
-                stage_a(b + 1)
-            if more and nquad == 0:
-                stage_b_open(nb)
-            for part in range(2):
-                if more:
-                    for i in (2 * part, 2 * part + 1):
-                        kh, phi = variants[i]
-                        stage_b_bank(nb, nquad, kh, phi, i == 0)
-                    if part == 1:
-                        stage_b_close(nb, nquad)
-                for m in range(4 * part, 4 * part + 4):
-                    stage_c(b, quad, m)
+        def statistics(b):
+            window_sums(b)
+            math_1(b)
+            math_root(b)
+            math_2(b)
+
+        for b in range(2):
+            for quad in range(2):
+                fwd(b, quad)
+                evac(b, quad)
+        squares(0, 0)
+        squares(0, 1)
+        squares(1, 0)
+        regroup_w(0, 1, "v")
+        regroup_w(1, 1, "g")
+        statistics(0)
+        squares(1, 1)
+        regroup_w(0, 0, "s")
+        regroup_w(1, 0, "s")
+        norm(0)
+        back_to_channels(0)
+        quantise_w(0, 1)
+        quantise_w(0, 0)
+        fix_quantise(0)
+        statistics(1)
+        quantise_w(1, 0)
+        quantise_w(1, 1)
+        norm(1)
+        for m in range(4):
+            multiply(0, m)
+        back_to_channels(1)
+        fwd(2, 0)
+        evac(2, 0)
+        norm(2)
+        fix_quantise(1)
+        for m in range(4, 8):
+            multiply(0, m)
+        for n in range(1, NCH):
+            fb, fq = (n + 4) // 2, (n + 4) % 2
+            pb, pq = (n + 3) // 2, (n + 3) % 2
+            sb = (n + 2) // 2
+            if pb < NB:
+                squares(pb, pq)
+            if n + 1 < NCH:
+                back_to_channels(n + 1)
+            if fb < NB:
+                fwd(fb, fq)
+                evac(fb, fq)
+            if n % 2 == 0 and sb < NB:
+                statistics(sb)
+            if n + 2 < NCH:
+                norm(n + 2)
+            if n + 1 < NCH:
+                fix_quantise(n + 1)
+            for m in range(8):
+                multiply(n, m)

@@ -64,24 +64,22 @@ def tile_norm_conv_t_kernel(tc, a, conv_kernel, out):
 
         identb = const.tile([P, P], BF16, name="identb")
         make_identity(nc, identb[:])
-        identf = const.tile([P, P], F32, name="identf")
-        make_identity(nc, identf[:])
-        diag = const.tile([P, 388], F32, name="diag")
+        diag = const.tile([P, 388], BF16, name="diag")
         nc.gpsimd.memset(diag[:], 0.0)
         shiftb = const.tile([P, P], BF16, name="shiftb")
         nc.vector.memset(shiftb[:], 0.0)
         nc.vector.tensor_copy(out=shiftb[:, 1:P], in_=identb[:, 0 : P - 1])
-        nc.vector.tensor_copy(out=diag[:, Z_IN : Z_IN + P], in_=identf[:])
-        pair = const.tile([P, 388], F32, name="pair")
+        nc.vector.tensor_copy(out=diag[:, Z_IN : Z_IN + P], in_=identb[:])
+        pair = const.tile([P, 388], BF16, name="pair")
         nc.vector.tensor_tensor(out=pair[:, 0:387], in0=diag[:, 0:387], in1=diag[:, 1:388], op=ALU.add)
-        band = const.tile([P, 356], F32, name="band")
+        band = const.tile([P, 356], BF16, name="band")
         nc.vector.tensor_tensor(out=band[:, 0:355], in0=pair[:, 0:355], in1=pair[:, 32:387], op=ALU.add)
-        band_odd = const.tile([P, 356], F32, name="band_odd")
+        band_odd = const.tile([P, 356], BF16, name="band_odd")
         nc.vector.tensor_copy(
             out=band_odd[:, 0:354].rearrange("p (k t) -> p k t", t=2),
             in_=band[:, 0:354].rearrange("p (k t) -> p k t", t=2)[:, :, 0:1].to_broadcast([P, 177, 2]),
         )
-        band_even = const.tile([P, 356], F32, name="band_even")
+        band_even = const.tile([P, 356], BF16, name="band_even")
         nc.vector.tensor_copy(
             out=band_even[:, 1:355].rearrange("p (k t) -> p k t", t=2),
             in_=band[:, 1:355].rearrange("p (k t) -> p k t", t=2)[:, :, 0:1].to_broadcast([P, 177, 2]),
@@ -116,6 +114,7 @@ def tile_norm_conv_t_kernel(tc, a, conv_kernel, out):
         sums = {}
         front = {}
         wins = {}
+        parts = {}
         means = {}
         rstds = {}
         devs = {}
@@ -158,16 +157,25 @@ def tile_norm_conv_t_kernel(tc, a, conv_kernel, out):
                     out=junk[:], in_=a_t[b][:, t, :], func=ACT.Square, accum_out=sums[b][:, 1, t + 1 : t + 2]
                 )
 
+        def split_sums(b, eng):
+            parts[b] = keep.tile([P, 3, 2, 16], BF16, name="parts%d" % b)
+            rest = small.tile([P, 2, 16], F32, name="rest")
+            eng.tensor_copy(out=parts[b][:, 0], in_=sums[b][:])
+            eng.tensor_tensor(out=rest[:], in0=sums[b][:], in1=parts[b][:, 0], op=ALU.subtract)
+            eng.tensor_copy(out=parts[b][:, 1], in_=rest[:])
+            eng.tensor_tensor(out=parts[b][:, 2], in0=rest[:], in1=parts[b][:, 1], op=ALU.subtract)
+
         def window_sums(b):
-            win = ps_w.tile([P, 4, 2, TPI], F32, name="win", tag="work")
+            win = ps_w.tile([P, 4, 6, TPI], F32, name="win", tag="work")
             wins[b] = win
+            src = parts[b][:].rearrange("p q s t -> p (q s) t")
             for v, (kh, phi) in enumerate(VARIANTS):
                 side = 1 if kh == 0 else -1
                 z0 = Z_IN - 32 * kh
                 nc.tensor.matmul(
                     out=win[:, v],
                     lhsT=bands[phi][:, z0 : z0 + P],
-                    rhs=sums[b][:, :, 1 : 1 + TPI],
+                    rhs=src[:, :, 1 : 1 + TPI],
                     start=True,
                     stop=False,
                 )
@@ -175,21 +183,27 @@ def tile_norm_conv_t_kernel(tc, a, conv_kernel, out):
                 nc.tensor.matmul(
                     out=win[:, v],
                     lhsT=bands[phi][:, z1 : z1 + P],
-                    rhs=sums[b][:, :, 1 + side : 1 + side + TPI],
+                    rhs=src[:, :, 1 + side : 1 + side + TPI],
                     start=False,
                     stop=True,
                 )
 
         def math_1(b):
-            win = wins[b]
+            tot = small.tile([P, 4, 2, TPI], F32, name="tot")
+            nc.vector.tensor_reduce(
+                out=tot[:].rearrange("p v s t -> p v (s t)"),
+                in_=wins[b][:].rearrange("p v (q s) t -> p v (s t) q", q=3),
+                axis=mybir.AxisListType.X,
+                op=ALU.add,
+            )
             means[b] = keep.tile([P, 4, TPI], F32, name="mean%d" % b)
             nc.vector.tensor_scalar(
-                out=means[b][:], in0=win[:, :, 0, :], scalar1=1.0 / 1024.0, scalar2=None, op0=ALU.mult
+                out=means[b][:], in0=tot[:, :, 0, :], scalar1=1.0 / 1024.0, scalar2=None, op0=ALU.mult
             )
             sq = small.tile([P, 4, TPI], F32, name="sq")
-            nc.vector.tensor_tensor(out=sq[:], in0=means[b][:], in1=win[:, :, 0, :], op=ALU.mult)
+            nc.vector.tensor_tensor(out=sq[:], in0=means[b][:], in1=tot[:, :, 0, :], op=ALU.mult)
             devs[b] = small.tile([P, 4, TPI], F32, name="dev")
-            nc.vector.tensor_tensor(out=devs[b][:], in0=win[:, :, 1, :], in1=sq[:], op=ALU.subtract)
+            nc.vector.tensor_tensor(out=devs[b][:], in0=tot[:, :, 1, :], in1=sq[:], op=ALU.subtract)
 
         def math_root(b):
             stds[b] = small.tile([P, 4, TPI], F32, name="std")
@@ -243,10 +257,12 @@ def tile_norm_conv_t_kernel(tc, a, conv_kernel, out):
             hi = 15 if (kh == 0 and quad == 1) else 16
             r0 = 16 * quad + lo + 1 - kh
             r1 = 16 * quad + hi + 1 - kh
-            nc.vector.tensor_copy(
-                out=grouped[b][:, kh, phi, r0:r1].rearrange("p i j (e k) -> p (i j) e k", e=2),
-                in_=back[(k, v)][:, :, 32 * lo : 32 * hi].rearrange("p e (x k) -> p x e k", k=2),
-            )
+            dst = grouped[b][:, kh, phi, r0:r1].rearrange("p i j (e k) -> p (i j) e k", e=2)
+            src = back[(k, v)][:, :, 32 * lo : 32 * hi].rearrange("p e (x k) -> p x e k", k=2)
+            if v == 0 and k >= 2:
+                nc.scalar.copy(out=dst, in_=src)
+            else:
+                nc.vector.tensor_copy(out=dst, in_=src)
 
         def fix_quantise(k):
             b, quad = k // 2, k % 2
@@ -282,9 +298,12 @@ def tile_norm_conv_t_kernel(tc, a, conv_kernel, out):
                     stop=(kh == 1),
                 )
             o_sb = opool.tile([P, 512], F32, name="o_sb")
-            nc.scalar.copy(
-                out=o_sb[:].rearrange("p (x f) -> p x f", f=2), in_=acc[:].rearrange("p (f x) -> p x f", f=2)
-            )
+            dst = o_sb[:].rearrange("p (x f) -> p x f", f=2)
+            src = acc[:].rearrange("p (f x) -> p x f", f=2)
+            if k == NCH - 1 and m % 2 == 1:
+                nc.vector.tensor_copy(out=dst, in_=src)
+            else:
+                nc.scalar.copy(out=dst, in_=src)
             nc.sync.dma_start(
                 out=out[b, P * m : P * m + P, 16 * quad : 16 * quad + 16, :].rearrange("o i j -> o (i j)"),
                 in_=o_sb[:],
@@ -296,6 +315,7 @@ def tile_norm_conv_t_kernel(tc, a, conv_kernel, out):
                 copy_out(k, v)
 
         def statistics(b):
+            split_sums(b, nc.vector if b == 0 else nc.gpsimd)
             window_sums(b)
             math_1(b)
             math_root(b)

@@ -29,7 +29,7 @@ def tile_norm_conv_t_kernel(tc, a, conv_kernel, out):
         small = ctx.enter_context(tc.tile_pool(name="small", bufs=2))
         npool = ctx.enter_context(tc.tile_pool(name="npool", bufs=8))
         gpool = ctx.enter_context(tc.tile_pool(name="gpool", bufs=2))
-        opool = ctx.enter_context(tc.tile_pool(name="opool", bufs=6))
+        opool = ctx.enter_context(tc.tile_pool(name="opool", bufs=12))
         ps_w = ctx.enter_context(tc.psum_pool(name="ps_w", bufs=5))
         ps_o = ctx.enter_context(tc.psum_pool(name="ps_o", bufs=3))
         ctx.enter_context(tc.manual_schedule())
@@ -64,22 +64,24 @@ def tile_norm_conv_t_kernel(tc, a, conv_kernel, out):
 
         identb = const.tile([P, P], BF16, name="identb")
         make_identity(nc, identb[:])
-        diag = const.tile([P, 388], BF16, name="diag")
+        identf = const.tile([P, P], F32, name="identf")
+        make_identity(nc, identf[:])
+        diag = const.tile([P, 388], F32, name="diag")
         nc.gpsimd.memset(diag[:], 0.0)
         shiftb = const.tile([P, P], BF16, name="shiftb")
         nc.vector.memset(shiftb[:], 0.0)
         nc.vector.tensor_copy(out=shiftb[:, 1:P], in_=identb[:, 0 : P - 1])
-        nc.vector.tensor_copy(out=diag[:, Z_IN : Z_IN + P], in_=identb[:])
-        pair = const.tile([P, 388], BF16, name="pair")
+        nc.vector.tensor_copy(out=diag[:, Z_IN : Z_IN + P], in_=identf[:])
+        pair = const.tile([P, 388], F32, name="pair")
         nc.vector.tensor_tensor(out=pair[:, 0:387], in0=diag[:, 0:387], in1=diag[:, 1:388], op=ALU.add)
-        band = const.tile([P, 356], BF16, name="band")
+        band = const.tile([P, 356], F32, name="band")
         nc.vector.tensor_tensor(out=band[:, 0:355], in0=pair[:, 0:355], in1=pair[:, 32:387], op=ALU.add)
-        band_odd = const.tile([P, 356], BF16, name="band_odd")
+        band_odd = const.tile([P, 356], F32, name="band_odd")
         nc.vector.tensor_copy(
             out=band_odd[:, 0:354].rearrange("p (k t) -> p k t", t=2),
             in_=band[:, 0:354].rearrange("p (k t) -> p k t", t=2)[:, :, 0:1].to_broadcast([P, 177, 2]),
         )
-        band_even = const.tile([P, 356], BF16, name="band_even")
+        band_even = const.tile([P, 356], F32, name="band_even")
         nc.vector.tensor_copy(
             out=band_even[:, 1:355].rearrange("p (k t) -> p k t", t=2),
             in_=band[:, 1:355].rearrange("p (k t) -> p k t", t=2)[:, :, 0:1].to_broadcast([P, 177, 2]),
@@ -114,7 +116,6 @@ def tile_norm_conv_t_kernel(tc, a, conv_kernel, out):
         sums = {}
         front = {}
         wins = {}
-        parts = {}
         means = {}
         rstds = {}
         devs = {}
@@ -157,25 +158,16 @@ def tile_norm_conv_t_kernel(tc, a, conv_kernel, out):
                     out=junk[:], in_=a_t[b][:, t, :], func=ACT.Square, accum_out=sums[b][:, 1, t + 1 : t + 2]
                 )
 
-        def split_sums(b, eng):
-            parts[b] = keep.tile([P, 3, 2, 16], BF16, name="parts%d" % b)
-            rest = small.tile([P, 2, 16], F32, name="rest")
-            eng.tensor_copy(out=parts[b][:, 0], in_=sums[b][:])
-            eng.tensor_tensor(out=rest[:], in0=sums[b][:], in1=parts[b][:, 0], op=ALU.subtract)
-            eng.tensor_copy(out=parts[b][:, 1], in_=rest[:])
-            eng.tensor_tensor(out=parts[b][:, 2], in0=rest[:], in1=parts[b][:, 1], op=ALU.subtract)
-
         def window_sums(b):
-            win = ps_w.tile([P, 4, 6, TPI], F32, name="win", tag="work")
+            win = ps_w.tile([P, 4, 2, TPI], F32, name="win", tag="work")
             wins[b] = win
-            src = parts[b][:].rearrange("p q s t -> p (q s) t")
             for v, (kh, phi) in enumerate(VARIANTS):
                 side = 1 if kh == 0 else -1
                 z0 = Z_IN - 32 * kh
                 nc.tensor.matmul(
                     out=win[:, v],
                     lhsT=bands[phi][:, z0 : z0 + P],
-                    rhs=src[:, :, 1 : 1 + TPI],
+                    rhs=sums[b][:, :, 1 : 1 + TPI],
                     start=True,
                     stop=False,
                 )
@@ -183,27 +175,21 @@ def tile_norm_conv_t_kernel(tc, a, conv_kernel, out):
                 nc.tensor.matmul(
                     out=win[:, v],
                     lhsT=bands[phi][:, z1 : z1 + P],
-                    rhs=src[:, :, 1 + side : 1 + side + TPI],
+                    rhs=sums[b][:, :, 1 + side : 1 + side + TPI],
                     start=False,
                     stop=True,
                 )
 
         def math_1(b):
-            tot = small.tile([P, 4, 2, TPI], F32, name="tot")
-            nc.vector.tensor_reduce(
-                out=tot[:].rearrange("p v s t -> p v (s t)"),
-                in_=wins[b][:].rearrange("p v (q s) t -> p v (s t) q", q=3),
-                axis=mybir.AxisListType.X,
-                op=ALU.add,
-            )
+            win = wins[b]
             means[b] = keep.tile([P, 4, TPI], F32, name="mean%d" % b)
             nc.vector.tensor_scalar(
-                out=means[b][:], in0=tot[:, :, 0, :], scalar1=1.0 / 1024.0, scalar2=None, op0=ALU.mult
+                out=means[b][:], in0=win[:, :, 0, :], scalar1=1.0 / 1024.0, scalar2=None, op0=ALU.mult
             )
             sq = small.tile([P, 4, TPI], F32, name="sq")
-            nc.vector.tensor_tensor(out=sq[:], in0=means[b][:], in1=tot[:, :, 0, :], op=ALU.mult)
+            nc.vector.tensor_tensor(out=sq[:], in0=means[b][:], in1=win[:, :, 0, :], op=ALU.mult)
             devs[b] = small.tile([P, 4, TPI], F32, name="dev")
-            nc.vector.tensor_tensor(out=devs[b][:], in0=tot[:, :, 1, :], in1=sq[:], op=ALU.subtract)
+            nc.vector.tensor_tensor(out=devs[b][:], in0=win[:, :, 1, :], in1=sq[:], op=ALU.subtract)
 
         def math_root(b):
             stds[b] = small.tile([P, 4, TPI], F32, name="std")
@@ -257,12 +243,10 @@ def tile_norm_conv_t_kernel(tc, a, conv_kernel, out):
             hi = 15 if (kh == 0 and quad == 1) else 16
             r0 = 16 * quad + lo + 1 - kh
             r1 = 16 * quad + hi + 1 - kh
-            dst = grouped[b][:, kh, phi, r0:r1].rearrange("p i j (e k) -> p (i j) e k", e=2)
-            src = back[(k, v)][:, :, 32 * lo : 32 * hi].rearrange("p e (x k) -> p x e k", k=2)
-            if v == 0 and k >= 2:
-                nc.scalar.copy(out=dst, in_=src)
-            else:
-                nc.vector.tensor_copy(out=dst, in_=src)
+            nc.vector.tensor_copy(
+                out=grouped[b][:, kh, phi, r0:r1].rearrange("p i j (e k) -> p (i j) e k", e=2),
+                in_=back[(k, v)][:, :, 32 * lo : 32 * hi].rearrange("p e (x k) -> p x e k", k=2),
+            )
 
         def fix_quantise(k):
             b, quad = k // 2, k % 2
@@ -298,12 +282,9 @@ def tile_norm_conv_t_kernel(tc, a, conv_kernel, out):
                     stop=(kh == 1),
                 )
             o_sb = opool.tile([P, 512], F32, name="o_sb")
-            dst = o_sb[:].rearrange("p (x f) -> p x f", f=2)
-            src = acc[:].rearrange("p (f x) -> p x f", f=2)
-            if k == NCH - 1 and m % 2 == 1:
-                nc.vector.tensor_copy(out=dst, in_=src)
-            else:
-                nc.scalar.copy(out=dst, in_=src)
+            nc.scalar.copy(
+                out=o_sb[:].rearrange("p (x f) -> p x f", f=2), in_=acc[:].rearrange("p (f x) -> p x f", f=2)
+            )
             nc.sync.dma_start(
                 out=out[b, P * m : P * m + P, 16 * quad : 16 * quad + 16, :].rearrange("o i j -> o (i j)"),
                 in_=o_sb[:],
@@ -315,7 +296,6 @@ def tile_norm_conv_t_kernel(tc, a, conv_kernel, out):
                 copy_out(k, v)
 
         def statistics(b):
-            split_sums(b, nc.vector if b == 0 else nc.gpsimd)
             window_sums(b)
             math_1(b)
             math_root(b)

@@ -48,7 +48,7 @@ def tile_norm_conv_t_kernel(tc, a, conv_kernel, out):
             cols = slice(512 * half, 512 * half + 512)
             for kh in range(2):
                 for e in range(2):
-                    nc.sync.dma_start(out=w_raw[:, kh, 2 * e : 2 * e + 2, cols], in_=w_view[:, e, kh, :, cols])
+                    nc.sync.dma_start(out=w_raw[:, kh, e:4:2, cols], in_=w_view[:, e, kh, :, cols])
 
         load_a(0)
         load_a(1)
@@ -68,9 +68,6 @@ def tile_norm_conv_t_kernel(tc, a, conv_kernel, out):
         make_identity(nc, identf[:])
         diag = const.tile([P, 388], F32, name="diag")
         nc.gpsimd.memset(diag[:], 0.0)
-        shiftb = const.tile([P, P], BF16, name="shiftb")
-        nc.vector.memset(shiftb[:], 0.0)
-        nc.vector.tensor_copy(out=shiftb[:, 1:P], in_=identb[:, 0 : P - 1])
         nc.vector.tensor_copy(out=diag[:, Z_IN : Z_IN + P], in_=identf[:])
         pair = const.tile([P, 388], F32, name="pair")
         nc.vector.tensor_tensor(out=pair[:, 0:387], in0=diag[:, 0:387], in1=diag[:, 1:388], op=ALU.add)
@@ -222,50 +219,51 @@ def tile_norm_conv_t_kernel(tc, a, conv_kernel, out):
                     )
 
         def bwd(k, v):
-            phi = VARIANTS[v][1]
-            bk = ps_w.tile([P, 2, 512], BF16, name="bk", tag="work")
+            bk = ps_w.tile([P, 512], F32, name="bk", tag="work")
             back[(k, v)] = bk
-            perm = identb if phi == 1 else shiftb
             for tl in range(4):
-                for e in range(2):
-                    nc.tensor.transpose(
-                        out=bk[:, e, P * tl : P * tl + P],
-                        in_=normed[(k, v)][:, tl, e:256:2],
-                        identity=perm[:],
-                    )
+                nc.tensor.transpose(
+                    out=bk[:, P * tl : P * tl + P],
+                    in_=normed[(k, v)][:, tl, :].bitcast(F32),
+                    identity=identf[:],
+                )
 
         def copy_out(k, v):
             b, quad = k // 2, k % 2
             kh, phi = VARIANTS[v]
             if quad == 0 and v == 0:
-                grouped[b] = gpool.tile([P, 2, 2, 32, 16, 4], BF16, name="grouped", align_bytes=64)
+                grouped[b] = gpool.tile([P, 2, 2, 2048], BF16, name="grouped", align_bytes=64)
             lo = 1 if (kh == 1 and quad == 0) else 0
             hi = 15 if (kh == 0 and quad == 1) else 16
-            r0 = 16 * quad + lo + 1 - kh
-            r1 = 16 * quad + hi + 1 - kh
+            d0 = 32 * (16 * quad + lo + 1 - kh)
+            n = 32 * (hi - lo)
+            s = 1 - phi
             nc.vector.tensor_copy(
-                out=grouped[b][:, kh, phi, r0:r1].rearrange("p i j (e k) -> p (i j) e k", e=2),
-                in_=back[(k, v)][:, :, 32 * lo : 32 * hi].rearrange("p e (x k) -> p x e k", k=2),
+                out=grouped[b][:, kh, phi, :].bitcast(F32)[:, d0 + s : d0 + n],
+                in_=back[(k, v)][:, 32 * lo : 32 * hi - s],
             )
 
         def fix_quantise(k):
             b, quad = k // 2, k % 2
             g = grouped[b]
+            words = g[:].rearrange("p h f x -> p (h f x)").bitcast(F32).rearrange(
+                "p (h f r x) -> p h f r x", h=2, f=2, r=32
+            )
             if quad == 0:
                 codes[b] = gpool.tile([P, 2, 2, 2, 256], U32, name="codes", align_bytes=64)
                 scales[b] = gpool.tile([P, 2, 2, 2, 256], U8, name="scales", align_bytes=64)
             r0 = 1 if quad == 0 else 16
             r1 = 16 * quad + 16
-            nc.vector.tensor_copy(out=g[:, :, 0, r0:r1, 0, 0:4:2], in_=g[:, :, 1, r0:r1, 0, 1:4:2])
+            nc.vector.tensor_copy(out=words[:, :, 0, r0:r1, 0], in_=words[:, :, 1, r0:r1, 1])
             if quad == 0:
                 for kh in range(2):
-                    nc.vector.tensor_copy(out=g[:, kh, :, 0], in_=g[:, 1 - kh, :, 1])
+                    nc.vector.tensor_copy(out=words[:, kh, :, 0], in_=words[:, 1 - kh, :, 1])
             for phi in (1, 0):
                 for kh in range(2):
                     nc.vector.quantize_mx(
                         out=codes[b][:, kh, quad, phi, :].bitcast(FP8X4),
                         scales=scales[b][:, kh, quad, phi, :],
-                        in_=g[:, kh, phi, 16 * quad : 16 * quad + 16].rearrange("p i j t -> p (i j t)"),
+                        in_=g[:, kh, phi, 1024 * quad : 1024 * quad + 1024],
                     )
 
         def multiply(k, m):

@@ -111,6 +111,7 @@ def tile_norm_conv_t_kernel(tc, a, conv_kernel, out):
 
         a_t = {}
         sums = {}
+        moments = {}
         front = {}
         wins = {}
         means = {}
@@ -123,6 +124,7 @@ def tile_norm_conv_t_kernel(tc, a, conv_kernel, out):
                 a_t[b] = keep.tile([P, TPI, 256], BF16, name="a_t%d" % b)
                 sums[b] = keep.tile([P, 2, 16], F32, name="sums%d" % b)
                 nc.vector.memset(sums[b][:], 0.0)
+                moments[b] = keep.tile([P, TPI, 6], F32, name="moments%d" % b)
             f_t = ps_w.tile([P, 4, 256], BF16, name="f_t", tag="work")
             front[(b, quad)] = f_t
             for tl in range(4):
@@ -135,25 +137,25 @@ def tile_norm_conv_t_kernel(tc, a, conv_kernel, out):
                     )
 
         def evac(b, quad):
-            for tl in range(4):
-                t = 4 * quad + tl
-                nc.vector.tensor_scalar(
-                    out=a_t[b][:, t, :],
-                    in0=front[(b, quad)][:, tl, :],
-                    scalar1=1.0,
-                    scalar2=None,
-                    op0=ALU.mult,
-                    op1=ALU.add,
-                    accum_out=sums[b][:, 0, t + 1 : t + 2],
-                )
+            nc.scalar.copy(out=a_t[b][:, 4 * quad : 4 * quad + 4, :], in_=front[(b, quad)][:])
 
-        def squares(b, quad):
-            for tl in range(4):
-                t = 4 * quad + tl
-                junk = small.tile([P, 256], BF16, name="junk")
-                nc.scalar.activation(
-                    out=junk[:], in_=a_t[b][:, t, :], func=ACT.Square, accum_out=sums[b][:, 1, t + 1 : t + 2]
-                )
+        def pixel_sums(b, quad):
+            ts = slice(4 * quad, 4 * quad + 4)
+            for t in range(4 * quad, 4 * quad + 4):
+                nc.vector.bn_stats(out=moments[b][:, t, :], in_=a_t[b][:, t, :])
+            mom = moments[b][:].rearrange("p t (e s) -> p t e s", e=2)
+            nc.vector.tensor_tensor(
+                out=sums[b][:, 0, 1 + 4 * quad : 5 + 4 * quad], in0=mom[:, ts, 0, 1], in1=mom[:, ts, 1, 1], op=ALU.add
+            )
+            m2 = small.tile([P, 4, 2], F32, name="m2")
+            nc.vector.tensor_tensor(out=m2[:], in0=mom[:, ts, :, 1], in1=mom[:, ts, :, 1], op=ALU.mult)
+            q2 = small.tile([P, 4, 2], F32, name="q2")
+            nc.vector.scalar_tensor_tensor(
+                out=q2[:], in0=m2[:], scalar=128.0, in1=mom[:, ts, :, 2], op0=ALU.mult, op1=ALU.add
+            )
+            nc.vector.tensor_tensor(
+                out=sums[b][:, 1, 1 + 4 * quad : 5 + 4 * quad], in0=q2[:, :, 0], in1=q2[:, :, 1], op=ALU.add
+            )
 
         def window_sums(b):
             win = ps_w.tile([P, 4, 2, TPI], F32, name="win", tag="work")
@@ -181,10 +183,12 @@ def tile_norm_conv_t_kernel(tc, a, conv_kernel, out):
             win = wins[b]
             means[b] = keep.tile([P, 4, TPI], F32, name="mean%d" % b)
             nc.vector.tensor_scalar(
-                out=means[b][:], in0=win[:, :, 0, :], scalar1=1.0 / 1024.0, scalar2=None, op0=ALU.mult
+                out=means[b][:], in0=win[:, :, 0, :], scalar1=0.125, scalar2=None, op0=ALU.mult
             )
             sq = small.tile([P, 4, TPI], F32, name="sq")
-            nc.vector.tensor_tensor(out=sq[:], in0=means[b][:], in1=win[:, :, 0, :], op=ALU.mult)
+            nc.vector.scalar_tensor_tensor(
+                out=sq[:], in0=means[b][:], scalar=128.0, in1=win[:, :, 0, :], op0=ALU.mult, op1=ALU.mult
+            )
             devs[b] = small.tile([P, 4, TPI], F32, name="dev")
             nc.vector.tensor_tensor(out=devs[b][:], in0=win[:, :, 1, :], in1=sq[:], op=ALU.subtract)
 
@@ -238,10 +242,12 @@ def tile_norm_conv_t_kernel(tc, a, conv_kernel, out):
             d0 = 32 * (16 * quad + lo + 1 - kh)
             n = 32 * (hi - lo)
             s = 1 - phi
-            nc.vector.tensor_copy(
-                out=grouped[b][:, kh, phi, :].bitcast(F32)[:, d0 + s : d0 + n],
-                in_=back[(k, v)][:, 32 * lo : 32 * hi - s],
-            )
+            dst = grouped[b][:, kh, phi, :].bitcast(F32)[:, d0 + s : d0 + n]
+            src = back[(k, v)][:, 32 * lo : 32 * hi - s]
+            if v % 2 == 0:
+                nc.vector.tensor_copy(out=dst, in_=src)
+            else:
+                nc.scalar.copy(out=dst, in_=src)
 
         def fix_quantise(k):
             b, quad = k // 2, k % 2
@@ -303,20 +309,20 @@ def tile_norm_conv_t_kernel(tc, a, conv_kernel, out):
             for quad in range(2):
                 fwd(b, quad)
                 evac(b, quad)
-        squares(0, 0)
-        squares(0, 1)
-        squares(1, 0)
-        regroup_w(0, 1, "v")
         regroup_w(1, 1, "g")
+        pixel_sums(0, 0)
+        pixel_sums(0, 1)
+        regroup_w(0, 1, "v")
         statistics(0)
-        squares(1, 1)
         regroup_w(0, 0, "s")
-        regroup_w(1, 0, "s")
         norm(0)
-        back_to_channels(0)
         quantise_w(0, 1)
+        back_to_channels(0)
         quantise_w(0, 0)
         fix_quantise(0)
+        regroup_w(1, 0, "s")
+        pixel_sums(1, 0)
+        pixel_sums(1, 1)
         statistics(1)
         quantise_w(1, 0)
         quantise_w(1, 1)
@@ -328,24 +334,31 @@ def tile_norm_conv_t_kernel(tc, a, conv_kernel, out):
         evac(2, 0)
         norm(2)
         fix_quantise(1)
+        pixel_sums(2, 0)
         for m in range(4, 8):
             multiply(0, m)
         for n in range(1, NCH):
             fb, fq = (n + 4) // 2, (n + 4) % 2
-            pb, pq = (n + 3) // 2, (n + 3) % 2
             sb = (n + 2) // 2
-            if pb < NB:
-                squares(pb, pq)
+            new_stats = n % 2 == 0 and sb < NB
             if n + 1 < NCH:
                 back_to_channels(n + 1)
             if fb < NB:
                 fwd(fb, fq)
                 evac(fb, fq)
-            if n % 2 == 0 and sb < NB:
-                statistics(sb)
-            if n + 2 < NCH:
-                norm(n + 2)
+            if new_stats:
+                window_sums(sb)
+                math_1(sb)
             if n + 1 < NCH:
                 fix_quantise(n + 1)
-            for m in range(8):
+            for m in range(2):
+                multiply(n, m)
+            if new_stats:
+                math_root(sb)
+                math_2(sb)
+            if n + 2 < NCH:
+                norm(n + 2)
+            if fb < NB:
+                pixel_sums(fb, fq)
+            for m in range(2, 8):
                 multiply(n, m)

@@ -66,19 +66,19 @@ def tile_norm_conv_t_kernel(tc, a, conv_kernel, out):
         make_identity(nc, identb[:])
         identf = const.tile([P, P], F32, name="identf")
         make_identity(nc, identf[:])
-        diag = const.tile([P, 388], F32, name="diag")
+        diag = const.tile([P, 388], BF16, name="diag")
         nc.gpsimd.memset(diag[:], 0.0)
-        nc.vector.tensor_copy(out=diag[:, Z_IN : Z_IN + P], in_=identf[:])
-        pair = const.tile([P, 388], F32, name="pair")
+        nc.vector.tensor_copy(out=diag[:, Z_IN : Z_IN + P], in_=identb[:])
+        pair = const.tile([P, 388], BF16, name="pair")
         nc.vector.tensor_tensor(out=pair[:, 0:387], in0=diag[:, 0:387], in1=diag[:, 1:388], op=ALU.add)
-        band = const.tile([P, 356], F32, name="band")
+        band = const.tile([P, 356], BF16, name="band")
         nc.vector.tensor_tensor(out=band[:, 0:355], in0=pair[:, 0:355], in1=pair[:, 32:387], op=ALU.add)
-        band_odd = const.tile([P, 356], F32, name="band_odd")
+        band_odd = const.tile([P, 356], BF16, name="band_odd")
         nc.vector.tensor_copy(
             out=band_odd[:, 0:354].rearrange("p (k t) -> p k t", t=2),
             in_=band[:, 0:354].rearrange("p (k t) -> p k t", t=2)[:, :, 0:1].to_broadcast([P, 177, 2]),
         )
-        band_even = const.tile([P, 356], F32, name="band_even")
+        band_even = const.tile([P, 356], BF16, name="band_even")
         nc.vector.tensor_copy(
             out=band_even[:, 1:355].rearrange("p (k t) -> p k t", t=2),
             in_=band[:, 1:355].rearrange("p (k t) -> p k t", t=2)[:, :, 0:1].to_broadcast([P, 177, 2]),
@@ -90,8 +90,8 @@ def tile_norm_conv_t_kernel(tc, a, conv_kernel, out):
         wc = keep.tile([P, 2, 1024], U32, name="wc", align_bytes=64)
         ws = keep.tile([P, 2, 1024], U8, name="ws", align_bytes=64)
 
-        def regroup_w(half, kh, engine):
-            cols = slice(512 * half, 512 * half + 512)
+        def regroup_w(half, kh, engine, part=slice(0, 512)):
+            cols = slice(512 * half + part.start, 512 * half + part.stop)
             dst = wg[:, kh, cols, :].rearrange("q (c i) t -> q c t i", i=4)
             src = w_raw[:, kh, :, cols].rearrange("q t (c i) -> q c t i", i=4)
             if engine == "v":
@@ -110,7 +110,7 @@ def tile_norm_conv_t_kernel(tc, a, conv_kernel, out):
             )
 
         a_t = {}
-        sums = {}
+        parts = {}
         moments = {}
         front = {}
         wins = {}
@@ -122,8 +122,8 @@ def tile_norm_conv_t_kernel(tc, a, conv_kernel, out):
         def fwd(b, quad):
             if quad == 0:
                 a_t[b] = keep.tile([P, TPI, 256], BF16, name="a_t%d" % b)
-                sums[b] = keep.tile([P, 2, 16], F32, name="sums%d" % b)
-                nc.vector.memset(sums[b][:], 0.0)
+                parts[b] = keep.tile([P, 6, 16], BF16, name="parts%d" % b)
+                nc.gpsimd.memset(parts[b][:], 0.0)
                 moments[b] = keep.tile([P, TPI, 6], F32, name="moments%d" % b)
             f_t = ps_w.tile([P, 4, 256], BF16, name="f_t", tag="work")
             front[(b, quad)] = f_t
@@ -139,58 +139,79 @@ def tile_norm_conv_t_kernel(tc, a, conv_kernel, out):
         def evac(b, quad):
             nc.scalar.copy(out=a_t[b][:, 4 * quad : 4 * quad + 4, :], in_=front[(b, quad)][:])
 
-        def pixel_sums(b, quad):
-            ts = slice(4 * quad, 4 * quad + 4)
-            for t in range(4 * quad, 4 * quad + 4):
-                nc.vector.bn_stats(out=moments[b][:, t, :], in_=a_t[b][:, t, :])
-            mom = moments[b][:].rearrange("p t (e s) -> p t e s", e=2)
-            nc.vector.tensor_tensor(
-                out=sums[b][:, 0, 1 + 4 * quad : 5 + 4 * quad], in0=mom[:, ts, 0, 1], in1=mom[:, ts, 1, 1], op=ALU.add
-            )
-            m2 = small.tile([P, 4, 2], F32, name="m2")
-            nc.vector.tensor_tensor(out=m2[:], in0=mom[:, ts, :, 1], in1=mom[:, ts, :, 1], op=ALU.mult)
-            q2 = small.tile([P, 4, 2], F32, name="q2")
-            nc.vector.scalar_tensor_tensor(
-                out=q2[:], in0=m2[:], scalar=128.0, in1=mom[:, ts, :, 2], op0=ALU.mult, op1=ALU.add
-            )
-            nc.vector.tensor_tensor(
-                out=sums[b][:, 1, 1 + 4 * quad : 5 + 4 * quad], in0=q2[:, :, 0], in1=q2[:, :, 1], op=ALU.add
-            )
+        def pixel_moments(b, quad):
+            return [
+                lambda t=t: nc.vector.bn_stats(out=moments[b][:, t, :], in_=a_t[b][:, t, :])
+                for t in range(4 * quad, 4 * quad + 4)
+            ]
+
+        def pixel_sums(b, t0, t1, eng):
+            n = t1 - t0
+            mom = moments[b][:, t0:t1, :].rearrange("p t (e s) -> p t e s", e=2)
+            mean, m2 = mom[:, :, :, 1], mom[:, :, :, 2]
+            tiles = {}
+            for name, shape in (("big", [P, n, 2]), ("sq2", [P, n, 2]), ("q2", [P, n, 2]), ("total", [P, 2, n]), ("rest", [P, 2, n])):
+                t = small.tile(shape, F32, name="%s_%d" % (name, n))
+                tiles[name] = t
+            big, sq2, q2, total, rest = [tiles[x][:] for x in ("big", "sq2", "q2", "total", "rest")]
+            hi, mid, lo = [parts[b][:, 2 * a : 2 * a + 2, 1 + t0 : 1 + t1] for a in range(3)]
+            return [
+                lambda: eng.tensor_scalar(out=big, in0=mean, scalar1=128.0, scalar2=0.0, op0=ALU.mult, op1=ALU.add),
+                lambda: eng.tensor_tensor(out=total[:, 0, :], in0=mean[:, :, 0], in1=mean[:, :, 1], op=ALU.add),
+                lambda: eng.tensor_tensor(out=sq2, in0=big, in1=mean, op=ALU.mult),
+                lambda: eng.tensor_tensor(out=q2, in0=sq2, in1=m2, op=ALU.add),
+                lambda: eng.tensor_tensor(out=total[:, 1, :], in0=q2[:, :, 0], in1=q2[:, :, 1], op=ALU.add),
+                lambda: eng.tensor_copy(out=hi, in_=total),
+                lambda: eng.tensor_tensor(out=rest, in0=total, in1=hi, op=ALU.subtract),
+                lambda: eng.tensor_copy(out=mid, in_=rest),
+                lambda: eng.tensor_tensor(out=lo, in0=rest, in1=mid, op=ALU.subtract),
+            ]
 
         def window_sums(b):
-            win = ps_w.tile([P, 4, 2, TPI], F32, name="win", tag="work")
+            win = ps_w.tile([P, 4, 48], F32, name="win", tag="work")
             wins[b] = win
             for v, (kh, phi) in enumerate(VARIANTS):
                 side = 1 if kh == 0 else -1
                 z0 = Z_IN - 32 * kh
+                dst = win[:, v].rearrange("p (x t) -> p x t", t=TPI)
                 nc.tensor.matmul(
-                    out=win[:, v],
+                    out=dst,
                     lhsT=bands[phi][:, z0 : z0 + P],
-                    rhs=sums[b][:, :, 1 : 1 + TPI],
+                    rhs=parts[b][:, :, 1 : 1 + TPI],
                     start=True,
                     stop=False,
                 )
                 z1 = z0 - P * side
                 nc.tensor.matmul(
-                    out=win[:, v],
+                    out=dst,
                     lhsT=bands[phi][:, z1 : z1 + P],
-                    rhs=sums[b][:, :, 1 + side : 1 + side + TPI],
+                    rhs=parts[b][:, :, 1 + side : 1 + side + TPI],
                     start=False,
                     stop=True,
                 )
 
         def math_1(b):
-            win = wins[b]
+            wsum = small.tile([P, 4, 16], F32, name="wsum")
             means[b] = keep.tile([P, 4, TPI], F32, name="mean%d" % b)
-            nc.vector.tensor_scalar(
-                out=means[b][:], in0=win[:, :, 0, :], scalar1=0.125, scalar2=None, op0=ALU.mult
-            )
             sq = small.tile([P, 4, TPI], F32, name="sq")
-            nc.vector.scalar_tensor_tensor(
-                out=sq[:], in0=means[b][:], scalar=128.0, in1=win[:, :, 0, :], op0=ALU.mult, op1=ALU.mult
-            )
             devs[b] = small.tile([P, 4, TPI], F32, name="dev")
-            nc.vector.tensor_tensor(out=devs[b][:], in0=win[:, :, 1, :], in1=sq[:], op=ALU.subtract)
+            return [
+                lambda: nc.vector.tensor_reduce(
+                    out=wsum[:],
+                    in_=wins[b][:].rearrange("p v (a x) -> p v x a", a=3),
+                    axis=mybir.AxisListType.X,
+                    op=ALU.add,
+                ),
+                lambda: nc.vector.tensor_scalar(
+                    out=means[b][:], in0=wsum[:, :, 0:TPI], scalar1=0.125, scalar2=None, op0=ALU.mult
+                ),
+                lambda: nc.vector.scalar_tensor_tensor(
+                    out=sq[:], in0=means[b][:], scalar=128.0, in1=wsum[:, :, 0:TPI], op0=ALU.mult, op1=ALU.mult
+                ),
+                lambda: nc.vector.tensor_tensor(
+                    out=devs[b][:], in0=wsum[:, :, TPI:16], in1=sq[:], op=ALU.subtract
+                ),
+            ]
 
         def math_root(b):
             stds[b] = small.tile([P, 4, TPI], F32, name="std")
@@ -208,19 +229,23 @@ def tile_norm_conv_t_kernel(tc, a, conv_kernel, out):
 
         def norm(k):
             b, quad = k // 2, k % 2
+            ops = []
             for v in range(4):
                 n_q = npool.tile([P, 4, 256], BF16, name="n_q")
                 normed[(k, v)] = n_q
                 for tl in range(4):
                     t = 4 * quad + tl
-                    nc.vector.tensor_scalar(
-                        out=n_q[:, tl, :],
-                        in0=a_t[b][:, t, :],
-                        scalar1=means[b][:, v, t : t + 1],
-                        scalar2=rstds[b][:, v, t : t + 1],
-                        op0=ALU.subtract,
-                        op1=ALU.mult,
+                    ops.append(
+                        lambda v=v, tl=tl, t=t, n_q=n_q: nc.vector.tensor_scalar(
+                            out=n_q[:, tl, :],
+                            in0=a_t[b][:, t, :],
+                            scalar1=means[b][:, v, t : t + 1],
+                            scalar2=rstds[b][:, v, t : t + 1],
+                            op0=ALU.subtract,
+                            op1=ALU.mult,
+                        )
                     )
+            return ops
 
         def bwd(k, v):
             bk = ps_w.tile([P, 512], F32, name="bk", tag="work")
@@ -299,66 +324,77 @@ def tile_norm_conv_t_kernel(tc, a, conv_kernel, out):
                 bwd(k, v)
                 copy_out(k, v)
 
-        def statistics(b):
-            window_sums(b)
-            math_1(b)
-            math_root(b)
-            math_2(b)
+        def run(ops, between=(), every=1):
+            done = 0
+            for i, op in enumerate(ops):
+                op()
+                if i % every == every - 1 and done < len(between):
+                    between[done]()
+                    done += 1
+            for op in between[done:]:
+                op()
 
         for b in range(2):
             for quad in range(2):
                 fwd(b, quad)
                 evac(b, quad)
         regroup_w(1, 1, "g")
-        pixel_sums(0, 0)
-        pixel_sums(0, 1)
-        regroup_w(0, 1, "v")
-        statistics(0)
+        run(pixel_moments(0, 0))
+        run(pixel_moments(0, 1), pixel_sums(0, 0, 4, nc.vector))
+        quarters = [lambda i=i: regroup_w(0, 1, "v", slice(128 * i, 128 * i + 128)) for i in range(4)]
+        run(pixel_sums(0, 4, 8, nc.vector), quarters, 2)
+        window_sums(0)
+        run(math_1(0))
+        math_root(0)
+        math_2(0)
         regroup_w(0, 0, "s")
-        norm(0)
+        run(norm(0))
         quantise_w(0, 1)
         back_to_channels(0)
         quantise_w(0, 0)
         fix_quantise(0)
         regroup_w(1, 0, "s")
-        pixel_sums(1, 0)
-        pixel_sums(1, 1)
-        statistics(1)
+        run(pixel_moments(1, 0))
+        run(pixel_moments(1, 1))
+        run(pixel_sums(1, 0, 8, nc.gpsimd))
+        run(norm(1))
         quantise_w(1, 0)
         quantise_w(1, 1)
-        norm(1)
         for m in range(4):
             multiply(0, m)
+        window_sums(1)
         back_to_channels(1)
         fwd(2, 0)
         evac(2, 0)
-        norm(2)
+        run(math_1(1))
+        math_root(1)
+        math_2(1)
+        run(norm(2))
         fix_quantise(1)
-        pixel_sums(2, 0)
+        run(pixel_moments(2, 0))
         for m in range(4, 8):
             multiply(0, m)
         for n in range(1, NCH):
             fb, fq = (n + 4) // 2, (n + 4) % 2
-            sb = (n + 2) // 2
-            new_stats = n % 2 == 0 and sb < NB
             if n + 1 < NCH:
                 back_to_channels(n + 1)
             if fb < NB:
                 fwd(fb, fq)
                 evac(fb, fq)
-            if new_stats:
-                window_sums(sb)
-                math_1(sb)
+                run(pixel_moments(fb, fq))
+                if fq == 1:
+                    run(pixel_sums(fb, 0, 8, nc.gpsimd))
+            if n + 2 < NCH:
+                run(norm(n + 2))
             if n + 1 < NCH:
                 fix_quantise(n + 1)
-            for m in range(2):
+            for m in range(6):
                 multiply(n, m)
-            if new_stats:
-                math_root(sb)
-                math_2(sb)
-            if n + 2 < NCH:
-                norm(n + 2)
-            if fb < NB:
-                pixel_sums(fb, fq)
-            for m in range(2, 8):
+            if fb < NB and fq == 1:
+                window_sums(fb)
+                run(math_1(fb))
+            for m in range(6, 8):
                 multiply(n, m)
+            if fb < NB and fq == 1:
+                math_root(fb)
+                math_2(fb)

@@ -51,9 +51,9 @@ def tile_norm_conv_t_kernel(tc, a, conv_kernel, out):
                     nc.sync.dma_start(out=w_raw[:, kh, e:4:2, cols], in_=w_view[:, e, kh, :, cols])
 
         load_a(0)
-        load_a(1)
         load_w(0)
         load_w(1)
+        load_a(1)
         load_a(2)
         load_a(3)
 
@@ -111,6 +111,7 @@ def tile_norm_conv_t_kernel(tc, a, conv_kernel, out):
 
         a_t = {}
         parts = {}
+        totals = {}
         moments = {}
         front = {}
         wins = {}
@@ -125,6 +126,7 @@ def tile_norm_conv_t_kernel(tc, a, conv_kernel, out):
                 parts[b] = keep.tile([P, 6, 16], BF16, name="parts%d" % b)
                 nc.gpsimd.memset(parts[b][:], 0.0)
                 moments[b] = keep.tile([P, TPI, 6], F32, name="moments%d" % b)
+                totals[b] = keep.tile([P, 2, TPI], F32, name="totals%d" % b)
             f_t = ps_w.tile([P, 4, 256], BF16, name="f_t", tag="work")
             front[(b, quad)] = f_t
             for tl in range(4):
@@ -139,32 +141,61 @@ def tile_norm_conv_t_kernel(tc, a, conv_kernel, out):
         def evac(b, quad):
             nc.scalar.copy(out=a_t[b][:, 4 * quad : 4 * quad + 4, :], in_=front[(b, quad)][:])
 
+        def evac_with_sums(b, quad):
+            for tl in range(4):
+                t = 4 * quad + tl
+                nc.scalar.activation(
+                    out=a_t[b][:, t, :],
+                    in_=front[(b, quad)][:, tl, :],
+                    func=ACT.Copy,
+                    accum_out=totals[b][:, 0, t : t + 1],
+                )
+
+        def squares(b, quad):
+            for t in range(4 * quad, 4 * quad + 4):
+                junk = small.tile([P, 256], BF16, name="junk")
+                nc.scalar.activation(
+                    out=junk[:], in_=a_t[b][:, t, :], func=ACT.Square, accum_out=totals[b][:, 1, t : t + 1]
+                )
+
         def pixel_moments(b, quad):
             return [
                 lambda t=t: nc.vector.bn_stats(out=moments[b][:, t, :], in_=a_t[b][:, t, :])
                 for t in range(4 * quad, 4 * quad + 4)
             ]
 
-        def pixel_sums(b, t0, t1, eng):
+        def pixel_sums(b, t0, t1):
             n = t1 - t0
+            total = totals[b]
             mom = moments[b][:, t0:t1, :].rearrange("p t (e s) -> p t e s", e=2)
             mean, m2 = mom[:, :, :, 1], mom[:, :, :, 2]
-            tiles = {}
-            for name, shape in (("big", [P, n, 2]), ("sq2", [P, n, 2]), ("q2", [P, n, 2]), ("total", [P, 2, n]), ("rest", [P, 2, n])):
-                t = small.tile(shape, F32, name="%s_%d" % (name, n))
-                tiles[name] = t
-            big, sq2, q2, total, rest = [tiles[x][:] for x in ("big", "sq2", "q2", "total", "rest")]
+            half = small.tile([P, n, 2], F32, name="half_%d" % n)
+            sq2 = small.tile([P, n, 2], F32, name="sq2_%d" % n)
+            q2 = small.tile([P, n, 2], F32, name="q2_%d" % n)
+            return [
+                lambda: nc.vector.tensor_scalar(out=half[:], in0=mean, scalar1=128.0, scalar2=None, op0=ALU.mult),
+                lambda: nc.vector.scalar_tensor_tensor(
+                    out=sq2[:], in0=mean, scalar=128.0, in1=mean, op0=ALU.mult, op1=ALU.mult
+                ),
+                lambda: nc.vector.tensor_tensor(
+                    out=total[:, 0, t0:t1], in0=half[:, :, 0], in1=half[:, :, 1], op=ALU.add
+                ),
+                lambda: nc.vector.tensor_tensor(out=q2[:], in0=sq2[:], in1=m2, op=ALU.add),
+                lambda: nc.vector.tensor_tensor(
+                    out=total[:, 1, t0:t1], in0=q2[:, :, 0], in1=q2[:, :, 1], op=ALU.add
+                ),
+            ]
+
+        def split_sums(b, t0, t1):
+            total = totals[b][:, :, t0:t1]
+            rest_t = small.tile([P, 2, t1 - t0], F32, name="rest_%d" % (t1 - t0))
+            rest = rest_t[:]
             hi, mid, lo = [parts[b][:, 2 * a : 2 * a + 2, 1 + t0 : 1 + t1] for a in range(3)]
             return [
-                lambda: eng.tensor_scalar(out=big, in0=mean, scalar1=128.0, scalar2=0.0, op0=ALU.mult, op1=ALU.add),
-                lambda: eng.tensor_tensor(out=total[:, 0, :], in0=mean[:, :, 0], in1=mean[:, :, 1], op=ALU.add),
-                lambda: eng.tensor_tensor(out=sq2, in0=big, in1=mean, op=ALU.mult),
-                lambda: eng.tensor_tensor(out=q2, in0=sq2, in1=m2, op=ALU.add),
-                lambda: eng.tensor_tensor(out=total[:, 1, :], in0=q2[:, :, 0], in1=q2[:, :, 1], op=ALU.add),
-                lambda: eng.tensor_copy(out=hi, in_=total),
-                lambda: eng.tensor_tensor(out=rest, in0=total, in1=hi, op=ALU.subtract),
-                lambda: eng.tensor_copy(out=mid, in_=rest),
-                lambda: eng.tensor_tensor(out=lo, in0=rest, in1=mid, op=ALU.subtract),
+                lambda: nc.vector.tensor_copy(out=hi, in_=total),
+                lambda: nc.vector.tensor_tensor(out=rest, in0=total, in1=hi, op=ALU.subtract),
+                lambda: nc.vector.tensor_copy(out=mid, in_=rest),
+                lambda: nc.vector.tensor_tensor(out=lo, in0=rest, in1=mid, op=ALU.subtract),
             ]
 
         def window_sums(b):
@@ -202,11 +233,16 @@ def tile_norm_conv_t_kernel(tc, a, conv_kernel, out):
                     axis=mybir.AxisListType.X,
                     op=ALU.add,
                 ),
-                lambda: nc.vector.tensor_scalar(
-                    out=means[b][:], in0=wsum[:, :, 0:TPI], scalar1=0.125, scalar2=None, op0=ALU.mult
-                ),
                 lambda: nc.vector.scalar_tensor_tensor(
-                    out=sq[:], in0=means[b][:], scalar=128.0, in1=wsum[:, :, 0:TPI], op0=ALU.mult, op1=ALU.mult
+                    out=sq[:],
+                    in0=wsum[:, :, 0:TPI],
+                    scalar=1.0 / 1024.0,
+                    in1=wsum[:, :, 0:TPI],
+                    op0=ALU.mult,
+                    op1=ALU.mult,
+                ),
+                lambda: nc.vector.tensor_scalar(
+                    out=means[b][:], in0=wsum[:, :, 0:TPI], scalar1=1.0 / 1024.0, scalar2=None, op0=ALU.mult
                 ),
                 lambda: nc.vector.tensor_tensor(
                     out=devs[b][:], in0=wsum[:, :, TPI:16], in1=sq[:], op=ALU.subtract
@@ -257,7 +293,7 @@ def tile_norm_conv_t_kernel(tc, a, conv_kernel, out):
                     identity=identf[:],
                 )
 
-        def copy_out(k, v):
+        def copy_out(k, v, engine):
             b, quad = k // 2, k % 2
             kh, phi = VARIANTS[v]
             if quad == 0 and v == 0:
@@ -269,7 +305,7 @@ def tile_norm_conv_t_kernel(tc, a, conv_kernel, out):
             s = 1 - phi
             dst = grouped[b][:, kh, phi, :].bitcast(F32)[:, d0 + s : d0 + n]
             src = back[(k, v)][:, 32 * lo : 32 * hi - s]
-            if v % 2 == 0:
+            if engine == "v":
                 nc.vector.tensor_copy(out=dst, in_=src)
             else:
                 nc.scalar.copy(out=dst, in_=src)
@@ -285,19 +321,22 @@ def tile_norm_conv_t_kernel(tc, a, conv_kernel, out):
                 scales[b] = gpool.tile([P, 2, 2, 2, 256], U8, name="scales", align_bytes=64)
             r0 = 1 if quad == 0 else 16
             r1 = 16 * quad + 16
-            nc.vector.tensor_copy(out=words[:, :, 0, r0:r1, 0], in_=words[:, :, 1, r0:r1, 1])
+            ops = [lambda: nc.vector.tensor_copy(out=words[:, :, 0, r0:r1, 0], in_=words[:, :, 1, r0:r1, 1])]
             if quad == 0:
                 for kh in range(2):
-                    nc.vector.tensor_copy(out=words[:, kh, :, 0], in_=words[:, 1 - kh, :, 1])
+                    ops.append(lambda kh=kh: nc.vector.tensor_copy(out=words[:, kh, :, 0], in_=words[:, 1 - kh, :, 1]))
             for phi in (1, 0):
                 for kh in range(2):
-                    nc.vector.quantize_mx(
-                        out=codes[b][:, kh, quad, phi, :].bitcast(FP8X4),
-                        scales=scales[b][:, kh, quad, phi, :],
-                        in_=g[:, kh, phi, 1024 * quad : 1024 * quad + 1024],
+                    ops.append(
+                        lambda phi=phi, kh=kh: nc.vector.quantize_mx(
+                            out=codes[b][:, kh, quad, phi, :].bitcast(FP8X4),
+                            scales=scales[b][:, kh, quad, phi, :],
+                            in_=g[:, kh, phi, 1024 * quad : 1024 * quad + 1024],
+                        )
                     )
+            return ops
 
-        def multiply(k, m):
+        def multiply(k, m, engine="s"):
             b, quad = k // 2, k % 2
             acc = ps_o.tile([P, 512], F32, name="acc")
             for kh in range(2):
@@ -311,18 +350,20 @@ def tile_norm_conv_t_kernel(tc, a, conv_kernel, out):
                     stop=(kh == 1),
                 )
             o_sb = opool.tile([P, 512], F32, name="o_sb")
-            nc.scalar.copy(
-                out=o_sb[:].rearrange("p (x f) -> p x f", f=2), in_=acc[:].rearrange("p (f x) -> p x f", f=2)
-            )
+            dst, src = o_sb[:].rearrange("p (x f) -> p x f", f=2), acc[:].rearrange("p (f x) -> p x f", f=2)
+            if engine == "v":
+                nc.vector.tensor_copy(out=dst, in_=src)
+            else:
+                nc.scalar.copy(out=dst, in_=src)
             nc.sync.dma_start(
                 out=out[b, P * m : P * m + P, 16 * quad : 16 * quad + 16, :].rearrange("o i j -> o (i j)"),
                 in_=o_sb[:],
             )
 
-        def back_to_channels(k):
+        def back_to_channels(k, engines="vsvs"):
             for v in range(4):
                 bwd(k, v)
-                copy_out(k, v)
+                copy_out(k, v, engines[v])
 
         def run(ops, between=(), every=1):
             done = 0
@@ -334,67 +375,84 @@ def tile_norm_conv_t_kernel(tc, a, conv_kernel, out):
             for op in between[done:]:
                 op()
 
-        for b in range(2):
-            for quad in range(2):
-                fwd(b, quad)
-                evac(b, quad)
-        regroup_w(1, 1, "g")
+        def pieces(half, kh, engine, n):
+            return [
+                lambda i=i: regroup_w(half, kh, engine, slice(512 // n * i, 512 // n * (i + 1))) for i in range(n)
+            ]
+
+        fwd(0, 0)
+        fwd(0, 1)
+        evac(0, 0)
+        evac_with_sums(0, 1)
+        squares(0, 1)
+        run(pieces(1, 0, "g", 8))
+        fwd(1, 0)
+        fwd(1, 1)
         run(pixel_moments(0, 0))
-        run(pixel_moments(0, 1), pixel_sums(0, 0, 4, nc.vector))
-        quarters = [lambda i=i: regroup_w(0, 1, "v", slice(128 * i, 128 * i + 128)) for i in range(4)]
-        run(pixel_sums(0, 4, 8, nc.vector), quarters, 2)
+        fill = pieces(0, 1, "v", 4) + pieces(0, 0, "v", 4)
+        run(pixel_sums(0, 0, 4), fill[0:4])
+        run(split_sums(0, 0, 8), fill[4:8])
         window_sums(0)
+        regroup_w(1, 1, "s")
+        quantise_w(0, 1)
         run(math_1(0))
         math_root(0)
-        math_2(0)
-        regroup_w(0, 0, "s")
-        run(norm(0))
-        quantise_w(0, 1)
-        back_to_channels(0)
         quantise_w(0, 0)
-        fix_quantise(0)
-        regroup_w(1, 0, "s")
-        run(pixel_moments(1, 0))
-        run(pixel_moments(1, 1))
-        run(pixel_sums(1, 0, 8, nc.gpsimd))
+        math_2(0)
+        run(norm(0))
+        evac_with_sums(1, 0)
+        back_to_channels(0, "vsvs")
+        run(fix_quantise(0))
+        evac_with_sums(1, 1)
+        squares(1, 0)
         run(norm(1))
         quantise_w(1, 0)
         quantise_w(1, 1)
-        for m in range(4):
+        for m in range(2):
             multiply(0, m)
-        window_sums(1)
+        squares(1, 1)
+        for m in range(2, 4):
+            multiply(0, m)
         back_to_channels(1)
         fwd(2, 0)
         evac(2, 0)
-        run(math_1(1))
-        math_root(1)
-        math_2(1)
-        run(norm(2))
-        fix_quantise(1)
-        run(pixel_moments(2, 0))
+        run(fix_quantise(1), split_sums(1, 0, 8), 1)
         for m in range(4, 8):
             multiply(0, m)
+        window_sums(1)
+        run(math_1(1))
+        math_root(1)
+        run(pixel_moments(2, 0))
+        math_2(1)
+        run(norm(2))
         for n in range(1, NCH):
             fb, fq = (n + 4) // 2, (n + 4) % 2
+            sb = (n + 2) // 2
+            new_stats = n % 2 == 0 and sb < NB
+            first = 4 if n < 2 else 2
+            for m in range(first):
+                multiply(n, m)
             if n + 1 < NCH:
-                back_to_channels(n + 1)
+                back_to_channels(n + 1, "vsvs")
+            if new_stats:
+                window_sums(sb)
+            moments_ops = []
             if fb < NB:
                 fwd(fb, fq)
                 evac(fb, fq)
-                run(pixel_moments(fb, fq))
-                if fq == 1:
-                    run(pixel_sums(fb, 0, 8, nc.gpsimd))
+                moments_ops = pixel_moments(fb, fq)
+            r = min(8, first + 3)
+            for m in range(first, r):
+                multiply(n, m)
+            fix = fix_quantise(n + 1) if n + 1 < NCH else []
+            math = math_1(sb) if new_stats else []
+            run(fix, math)
+            if new_stats:
+                math_root(sb)
+            run(moments_ops)
+            if new_stats:
+                math_2(sb)
             if n + 2 < NCH:
-                run(norm(n + 2))
-            if n + 1 < NCH:
-                fix_quantise(n + 1)
-            for m in range(6):
+                run(norm(n + 2), pixel_sums(fb, 0, 8) + split_sums(fb, 0, 8) if fb < NB and fq == 1 else [], 2)
+            for m in range(r, 8):
                 multiply(n, m)
-            if fb < NB and fq == 1:
-                window_sums(fb)
-                run(math_1(fb))
-            for m in range(6, 8):
-                multiply(n, m)
-            if fb < NB and fq == 1:
-                math_root(fb)
-                math_2(fb)

@@ -62,6 +62,8 @@ def tile_norm_conv_t_kernel(tc, a, conv_kernel, out):
         one_rt = const.tile([P, 1], F32, name="one_rt")
         nc.scalar.activation(out=one_rt[:], in_=one[:], func=ACT.Sqrt)
 
+        zeros = const.tile([P, 512], BF16, name="zeros")
+        nc.vector.memset(zeros[:], 0.0)
         identb = const.tile([P, P], BF16, name="identb")
         make_identity(nc, identb[:])
         identf = const.tile([P, P], F32, name="identf")
@@ -119,6 +121,11 @@ def tile_norm_conv_t_kernel(tc, a, conv_kernel, out):
         rstds = {}
         devs = {}
         stds = {}
+
+        def keep_busy(n):
+            idle = ps_w.tile([P, 512], F32, name="idle", tag="work")
+            for i in range(n):
+                nc.tensor.matmul(out=idle[:], lhsT=zeros[:, 0:P], rhs=zeros[:], start=True, stop=True)
 
         def fwd(b, quad):
             if quad == 0:
@@ -380,8 +387,10 @@ def tile_norm_conv_t_kernel(tc, a, conv_kernel, out):
                 lambda i=i: regroup_w(half, kh, engine, slice(512 // n * i, 512 // n * (i + 1))) for i in range(n)
             ]
 
+        keep_busy(5)
         fwd(0, 0)
         fwd(0, 1)
+        keep_busy(10)
         evac(0, 0)
         evac_with_sums(0, 1)
         squares(0, 1)
@@ -393,6 +402,7 @@ def tile_norm_conv_t_kernel(tc, a, conv_kernel, out):
         run(pixel_sums(0, 0, 4), fill[0:4])
         run(split_sums(0, 0, 8), fill[4:8])
         window_sums(0)
+        keep_busy(6)
         regroup_w(1, 1, "s")
         quantise_w(0, 1)
         run(math_1(0))
@@ -402,6 +412,7 @@ def tile_norm_conv_t_kernel(tc, a, conv_kernel, out):
         run(norm(0))
         evac_with_sums(1, 0)
         back_to_channels(0, "vsvs")
+        keep_busy(8)
         run(fix_quantise(0))
         evac_with_sums(1, 1)
         squares(1, 0)

@@ -38,19 +38,26 @@ def tile_norm_conv_t_kernel(tc, a, conv_kernel, out):
         for b in range(NB):
             a_b = keep.tile([P, 2, 1024], BF16, name="a_sb%d" % b)
             a_sb.append(a_b)
-        w_raw = keep.tile([P, 2, 4, 1024], BF16, name="w_raw")
+        w_raw = {}
+        for half in range(2):
+            for kh in range(2):
+                w_part = keep.tile([P, 4, 512], BF16, name="w_raw%d%d" % (half, kh))
+                w_raw[(half, kh)] = w_part
         w_view = conv_kernel.rearrange("(q e k w) o -> q e k w o", e=2, k=2, w=2)
 
-        def load_a(b):
-            nc.sync.dma_start(out=a_sb[b][:], in_=a[b].rearrange("(h c) i j -> c h (i j)", h=2))
+        def load_a(b, n=1):
+            a_view = a[b].rearrange("(h c) i j -> c h (i j)", h=2)
+            for i in range(n):
+                pixels = slice(1024 // n * i, 1024 // n * (i + 1))
+                nc.sync.dma_start(out=a_sb[b][:, :, pixels], in_=a_view[:, :, pixels])
 
         def load_w(half):
             cols = slice(512 * half, 512 * half + 512)
             for kh in range(2):
                 for e in range(2):
-                    nc.sync.dma_start(out=w_raw[:, kh, e:4:2, cols], in_=w_view[:, e, kh, :, cols])
+                    nc.sync.dma_start(out=w_raw[(half, kh)][:, e:4:2, :], in_=w_view[:, e, kh, :, cols])
 
-        load_a(0)
+        load_a(0, 2)
         load_w(0)
         load_w(1)
         load_a(1)
@@ -60,7 +67,7 @@ def tile_norm_conv_t_kernel(tc, a, conv_kernel, out):
         one = const.tile([P, 1], F32, name="one")
         nc.vector.memset(one[:], 1.0)
         one_rt = const.tile([P, 1], F32, name="one_rt")
-        nc.scalar.activation(out=one_rt[:], in_=one[:], func=ACT.Sqrt)
+        nc.scalar.activation(out=one_rt[:], in_=one[:], func=ACT.Abs_reciprocal_sqrt)
 
         zeros = const.tile([P, 512], BF16, name="zeros")
         nc.vector.memset(zeros[:], 0.0)
@@ -70,22 +77,20 @@ def tile_norm_conv_t_kernel(tc, a, conv_kernel, out):
         make_identity(nc, identf[:])
         diag = const.tile([P, 388], BF16, name="diag")
         nc.gpsimd.memset(diag[:], 0.0)
-        nc.vector.tensor_copy(out=diag[:, Z_IN : Z_IN + P], in_=identb[:])
+        def move(out, in_):
+            nc.gpsimd.tensor_scalar(out=out, in0=in_, scalar1=1.0, scalar2=0.0, op0=ALU.mult, op1=ALU.add)
+
+        move(diag[:, Z_IN : Z_IN + P], identb[:])
         pair = const.tile([P, 388], BF16, name="pair")
-        nc.vector.tensor_tensor(out=pair[:, 0:387], in0=diag[:, 0:387], in1=diag[:, 1:388], op=ALU.add)
+        nc.gpsimd.tensor_tensor(out=pair[:, 0:387], in0=diag[:, 0:387], in1=diag[:, 1:388], op=ALU.add)
         band = const.tile([P, 356], BF16, name="band")
-        nc.vector.tensor_tensor(out=band[:, 0:355], in0=pair[:, 0:355], in1=pair[:, 32:387], op=ALU.add)
+        nc.gpsimd.tensor_tensor(out=band[:, 0:355], in0=pair[:, 0:355], in1=pair[:, 32:387], op=ALU.add)
         band_odd = const.tile([P, 356], BF16, name="band_odd")
-        nc.vector.tensor_copy(
-            out=band_odd[:, 0:354].rearrange("p (k t) -> p k t", t=2),
-            in_=band[:, 0:354].rearrange("p (k t) -> p k t", t=2)[:, :, 0:1].to_broadcast([P, 177, 2]),
-        )
         band_even = const.tile([P, 356], BF16, name="band_even")
-        nc.vector.tensor_copy(
-            out=band_even[:, 1:355].rearrange("p (k t) -> p k t", t=2),
-            in_=band[:, 1:355].rearrange("p (k t) -> p k t", t=2)[:, :, 0:1].to_broadcast([P, 177, 2]),
-        )
-        nc.vector.tensor_copy(out=band_even[:, 2:354:32], in_=band[:, 2:354:32])
+        for t in range(2):
+            move(band_odd[:, t:354:2], band[:, 0:354:2])
+            move(band_even[:, 1 + t : 355 : 2], band[:, 1:355:2])
+        move(band_even[:, 2:354:32], band[:, 2:354:32])
         bands = [band_even, band_odd]
 
         wg = keep.tile([P, 2, 1024, 4], BF16, name="wg", align_bytes=64)
@@ -95,7 +100,7 @@ def tile_norm_conv_t_kernel(tc, a, conv_kernel, out):
         def regroup_w(half, kh, engine, part=slice(0, 512)):
             cols = slice(512 * half + part.start, 512 * half + part.stop)
             dst = wg[:, kh, cols, :].rearrange("q (c i) t -> q c t i", i=4)
-            src = w_raw[:, kh, :, cols].rearrange("q t (c i) -> q c t i", i=4)
+            src = w_raw[(half, kh)][:, :, part].rearrange("q t (c i) -> q c t i", i=4)
             if engine == "v":
                 nc.vector.tensor_copy(out=dst, in_=src)
             elif engine == "s":
@@ -120,7 +125,10 @@ def tile_norm_conv_t_kernel(tc, a, conv_kernel, out):
         means = {}
         rstds = {}
         devs = {}
-        stds = {}
+
+        for b in range(NB):
+            parts[b] = keep.tile([P, 6, 16], BF16, name="parts%d" % b)
+            nc.vector.memset(parts[b][:], 0.0)
 
         def keep_busy(n):
             idle = ps_w.tile([P, 512], F32, name="idle", tag="work")
@@ -130,8 +138,6 @@ def tile_norm_conv_t_kernel(tc, a, conv_kernel, out):
         def fwd(b, quad):
             if quad == 0:
                 a_t[b] = keep.tile([P, TPI, 256], BF16, name="a_t%d" % b)
-                parts[b] = keep.tile([P, 6, 16], BF16, name="parts%d" % b)
-                nc.gpsimd.memset(parts[b][:], 0.0)
                 moments[b] = keep.tile([P, TPI, 6], F32, name="moments%d" % b)
                 totals[b] = keep.tile([P, 2, TPI], F32, name="totals%d" % b)
             f_t = ps_w.tile([P, 4, 256], BF16, name="f_t", tag="work")
@@ -165,10 +171,13 @@ def tile_norm_conv_t_kernel(tc, a, conv_kernel, out):
                     out=junk[:], in_=a_t[b][:, t, :], func=ACT.Square, accum_out=totals[b][:, 1, t : t + 1]
                 )
 
-        def pixel_moments(b, quad):
+        def pixel_moments(b, quad, from_bank=False):
             return [
-                lambda t=t: nc.vector.bn_stats(out=moments[b][:, t, :], in_=a_t[b][:, t, :])
-                for t in range(4 * quad, 4 * quad + 4)
+                lambda tl=tl: nc.vector.bn_stats(
+                    out=moments[b][:, 4 * quad + tl, :],
+                    in_=front[(b, quad)][:, tl, :] if from_bank else a_t[b][:, 4 * quad + tl, :],
+                )
+                for tl in range(4)
             ]
 
         def pixel_sums(b, t0, t1):
@@ -257,12 +266,8 @@ def tile_norm_conv_t_kernel(tc, a, conv_kernel, out):
             ]
 
         def math_root(b):
-            stds[b] = small.tile([P, 4, TPI], F32, name="std")
-            nc.scalar.activation(out=stds[b][:], in_=devs[b][:], func=ACT.Sqrt, scale=1.0 / 1023.0)
-
-        def math_2(b):
             rstds[b] = keep.tile([P, 4, TPI], F32, name="rstd%d" % b)
-            nc.vector.reciprocal(out=rstds[b][:], in_=stds[b][:])
+            nc.scalar.activation(out=rstds[b][:], in_=devs[b][:], func=ACT.Abs_reciprocal_sqrt, scale=1.0 / 1023.0)
 
         grouped = {}
         codes = {}
@@ -387,28 +392,27 @@ def tile_norm_conv_t_kernel(tc, a, conv_kernel, out):
                 lambda i=i: regroup_w(half, kh, engine, slice(512 // n * i, 512 // n * (i + 1))) for i in range(n)
             ]
 
-        keep_busy(5)
+        keep_busy(3)
         fwd(0, 0)
         fwd(0, 1)
         keep_busy(10)
-        evac(0, 0)
         evac_with_sums(0, 1)
+        run(pixel_moments(0, 0, True))
         squares(0, 1)
+        evac(0, 0)
         run(pieces(1, 0, "g", 8))
-        fwd(1, 0)
-        fwd(1, 1)
-        run(pixel_moments(0, 0))
-        fill = pieces(0, 1, "v", 4) + pieces(0, 0, "v", 4)
+        fill = pieces(0, 0, "v", 4) + pieces(0, 1, "v", 4)
         run(pixel_sums(0, 0, 4), fill[0:4])
         run(split_sums(0, 0, 8), fill[4:8])
         window_sums(0)
-        keep_busy(6)
+        fwd(1, 0)
+        fwd(1, 1)
+        keep_busy(2)
         regroup_w(1, 1, "s")
-        quantise_w(0, 1)
+        quantise_w(0, 0)
         run(math_1(0))
         math_root(0)
-        quantise_w(0, 0)
-        math_2(0)
+        quantise_w(0, 1)
         run(norm(0))
         evac_with_sums(1, 0)
         back_to_channels(0, "vsvs")
@@ -424,23 +428,24 @@ def tile_norm_conv_t_kernel(tc, a, conv_kernel, out):
         squares(1, 1)
         for m in range(2, 4):
             multiply(0, m)
-        back_to_channels(1)
+        back_to_channels(1, "vvvs")
         fwd(2, 0)
         evac(2, 0)
         run(fix_quantise(1), split_sums(1, 0, 8), 1)
-        for m in range(4, 8):
+        for m in range(4, 7):
             multiply(0, m)
         window_sums(1)
+        for m in range(7, 8):
+            multiply(0, m)
         run(math_1(1))
         math_root(1)
         run(pixel_moments(2, 0))
-        math_2(1)
         run(norm(2))
         for n in range(1, NCH):
             fb, fq = (n + 4) // 2, (n + 4) % 2
             sb = (n + 2) // 2
             new_stats = n % 2 == 0 and sb < NB
-            first = 4 if n < 2 else 2
+            first = 4 if n < 3 else 2
             for m in range(first):
                 multiply(n, m)
             if n + 1 < NCH:
@@ -461,8 +466,6 @@ def tile_norm_conv_t_kernel(tc, a, conv_kernel, out):
             if new_stats:
                 math_root(sb)
             run(moments_ops)
-            if new_stats:
-                math_2(sb)
             if n + 2 < NCH:
                 run(norm(n + 2), pixel_sums(fb, 0, 8) + split_sums(fb, 0, 8) if fb < NB and fq == 1 else [], 2)
             for m in range(r, 8):

@@ -59,8 +59,8 @@ def tile_norm_conv_t_kernel(tc, a, conv_kernel, out):
 
         load_a(0, 2)
         load_w(0)
-        load_w(1)
         load_a(1)
+        load_w(1)
         load_a(2)
         load_a(3)
 
@@ -395,42 +395,45 @@ def tile_norm_conv_t_kernel(tc, a, conv_kernel, out):
         keep_busy(3)
         fwd(0, 0)
         fwd(0, 1)
-        keep_busy(10)
+        keep_busy(6)
+        fwd(1, 0)
+        fwd(1, 1)
         evac_with_sums(0, 1)
         run(pixel_moments(0, 0, True))
         squares(0, 1)
         evac(0, 0)
         run(pieces(1, 0, "g", 8))
+        run(pieces(1, 1, "g", 4)[0:2])
         fill = pieces(0, 0, "v", 4) + pieces(0, 1, "v", 4)
         run(pixel_sums(0, 0, 4), fill[0:4])
         run(split_sums(0, 0, 8), fill[4:8])
         window_sums(0)
-        fwd(1, 0)
-        fwd(1, 1)
         keep_busy(2)
-        regroup_w(1, 1, "s")
+        evac_with_sums(1, 0)
+        evac_with_sums(1, 1)
         quantise_w(0, 0)
         run(math_1(0))
         math_root(0)
         quantise_w(0, 1)
         run(norm(0))
-        evac_with_sums(1, 0)
-        back_to_channels(0, "vsvs")
-        keep_busy(8)
-        run(fix_quantise(0))
-        evac_with_sums(1, 1)
         squares(1, 0)
+        back_to_channels(0, "vsvs")
+        fwd(2, 0)
+        fwd(2, 1)
+        keep_busy(3)
+        run(fix_quantise(0))
+        squares(1, 1)
+        run(pieces(1, 1, "s", 4)[2:4])
         run(norm(1))
         quantise_w(1, 0)
         quantise_w(1, 1)
         for m in range(2):
             multiply(0, m)
-        squares(1, 1)
+        evac(2, 0)
         for m in range(2, 4):
             multiply(0, m)
         back_to_channels(1, "vvvs")
-        fwd(2, 0)
-        evac(2, 0)
+        evac(2, 1)
         run(fix_quantise(1), split_sums(1, 0, 8), 1)
         for m in range(4, 7):
             multiply(0, m)
@@ -450,13 +453,12 @@ def tile_norm_conv_t_kernel(tc, a, conv_kernel, out):
                 multiply(n, m)
             if n + 1 < NCH:
                 back_to_channels(n + 1, "vsvs")
+            if n + 5 < NCH:
+                fwd((n + 5) // 2, (n + 5) % 2)
+                evac((n + 5) // 2, (n + 5) % 2)
             if new_stats:
                 window_sums(sb)
-            moments_ops = []
-            if fb < NB:
-                fwd(fb, fq)
-                evac(fb, fq)
-                moments_ops = pixel_moments(fb, fq)
+            moments_ops = pixel_moments(fb, fq) if fb < NB else []
             r = min(8, first + 3)
             for m in range(first, r):
                 multiply(n, m)

@@ -73,25 +73,27 @@ def tile_norm_conv_t_kernel(tc, a, conv_kernel, out):
         nc.vector.memset(zeros[:], 0.0)
         identb = const.tile([P, P], BF16, name="identb")
         make_identity(nc, identb[:])
-        identf = const.tile([P, P], F32, name="identf")
-        make_identity(nc, identf[:])
         diag = const.tile([P, 388], BF16, name="diag")
-        nc.gpsimd.memset(diag[:], 0.0)
-        def move(out, in_):
-            nc.gpsimd.tensor_scalar(out=out, in0=in_, scalar1=1.0, scalar2=0.0, op0=ALU.mult, op1=ALU.add)
-
-        move(diag[:, Z_IN : Z_IN + P], identb[:])
+        nc.vector.memset(diag[:], 0.0)
+        nc.vector.tensor_copy(out=diag[:, Z_IN : Z_IN + P], in_=identb[:])
         pair = const.tile([P, 388], BF16, name="pair")
-        nc.gpsimd.tensor_tensor(out=pair[:, 0:387], in0=diag[:, 0:387], in1=diag[:, 1:388], op=ALU.add)
+        nc.vector.tensor_tensor(out=pair[:, 0:387], in0=diag[:, 0:387], in1=diag[:, 1:388], op=ALU.add)
         band = const.tile([P, 356], BF16, name="band")
-        nc.gpsimd.tensor_tensor(out=band[:, 0:355], in0=pair[:, 0:355], in1=pair[:, 32:387], op=ALU.add)
+        nc.vector.tensor_tensor(out=band[:, 0:355], in0=pair[:, 0:355], in1=pair[:, 32:387], op=ALU.add)
         band_odd = const.tile([P, 356], BF16, name="band_odd")
         band_even = const.tile([P, 356], BF16, name="band_even")
-        for t in range(2):
-            move(band_odd[:, t:354:2], band[:, 0:354:2])
-            move(band_even[:, 1 + t : 355 : 2], band[:, 1:355:2])
-        move(band_even[:, 2:354:32], band[:, 2:354:32])
+        nc.scalar.copy(
+            out=band_odd[:, 0:354].rearrange("p (k t) -> p k t", t=2),
+            in_=band[:, 0:354].rearrange("p (k t) -> p k t", t=2)[:, :, 0:1].to_broadcast([P, 177, 2]),
+        )
+        nc.scalar.copy(
+            out=band_even[:, 1:355].rearrange("p (k t) -> p k t", t=2),
+            in_=band[:, 1:355].rearrange("p (k t) -> p k t", t=2)[:, :, 0:1].to_broadcast([P, 177, 2]),
+        )
+        nc.scalar.copy(out=band_even[:, 2:354:32], in_=band[:, 2:354:32])
         bands = [band_even, band_odd]
+        identf = const.tile([P, P], F32, name="identf")
+        make_identity(nc, identf[:])
 
         wg = keep.tile([P, 2, 1024, 4], BF16, name="wg", align_bytes=64)
         wc = keep.tile([P, 2, 1024], U32, name="wc", align_bytes=64)
@@ -402,13 +404,11 @@ def tile_norm_conv_t_kernel(tc, a, conv_kernel, out):
         run(pixel_moments(0, 0, True))
         squares(0, 1)
         evac(0, 0)
-        run(pieces(1, 0, "g", 8))
-        run(pieces(1, 1, "g", 4)[0:2])
         fill = pieces(0, 0, "v", 4) + pieces(0, 1, "v", 4)
         run(pixel_sums(0, 0, 4), fill[0:4])
         run(split_sums(0, 0, 8), fill[4:8])
         window_sums(0)
-        keep_busy(2)
+        keep_busy(4)
         evac_with_sums(1, 0)
         evac_with_sums(1, 1)
         quantise_w(0, 0)
@@ -418,13 +418,15 @@ def tile_norm_conv_t_kernel(tc, a, conv_kernel, out):
         run(norm(0))
         squares(1, 0)
         back_to_channels(0, "vsvs")
+        keep_busy(2)
         fwd(2, 0)
         fwd(2, 1)
-        keep_busy(3)
+        keep_busy(2)
         run(fix_quantise(0))
         squares(1, 1)
-        run(pieces(1, 1, "s", 4)[2:4])
+        regroup_w(1, 1, "s")
         run(norm(1))
+        run(pieces(1, 0, "v", 4))
         quantise_w(1, 0)
         quantise_w(1, 1)
         for m in range(2):
@@ -432,8 +434,8 @@ def tile_norm_conv_t_kernel(tc, a, conv_kernel, out):
         evac(2, 0)
         for m in range(2, 4):
             multiply(0, m)
-        back_to_channels(1, "vvvs")
         evac(2, 1)
+        back_to_channels(1, "vvvs")
         run(fix_quantise(1), split_sums(1, 0, 8), 1)
         for m in range(4, 7):
             multiply(0, m)
@@ -449,26 +451,31 @@ def tile_norm_conv_t_kernel(tc, a, conv_kernel, out):
             sb = (n + 2) // 2
             new_stats = n % 2 == 0 and sb < NB
             first = 4 if n < 3 else 2
+            r = first + 1
             for m in range(first):
                 multiply(n, m)
-            if n + 1 < NCH:
-                back_to_channels(n + 1, "vsvs")
-            if n + 5 < NCH:
-                fwd((n + 5) // 2, (n + 5) % 2)
-                evac((n + 5) // 2, (n + 5) % 2)
+            math = []
             if new_stats:
                 window_sums(sb)
-            moments_ops = pixel_moments(fb, fq) if fb < NB else []
-            r = min(8, first + 3)
+                math = math_1(sb)
+                run(math[0:1])
+            if n + 1 < NCH:
+                back_to_channels(n + 1, "vsvs")
             for m in range(first, r):
                 multiply(n, m)
             fix = fix_quantise(n + 1) if n + 1 < NCH else []
-            math = math_1(sb) if new_stats else []
-            run(fix, math)
+            moments_ops = pixel_moments(fb, fq) if fb < NB else []
+            sums = pixel_sums(fb, 0, 8) + split_sums(fb, 0, 8) if fb < NB and fq == 1 else []
             if new_stats:
+                run(moments_ops, math[1:])
                 math_root(sb)
-            run(moments_ops)
+            else:
+                run(moments_ops)
+            run(fix, sums)
             if n + 2 < NCH:
-                run(norm(n + 2), pixel_sums(fb, 0, 8) + split_sums(fb, 0, 8) if fb < NB and fq == 1 else [], 2)
+                run(norm(n + 2))
+            if n + 5 < NCH:
+                fwd((n + 5) // 2, (n + 5) % 2)
+                evac((n + 5) // 2, (n + 5) % 2)
             for m in range(r, 8):
                 multiply(n, m)

@@ -397,7 +397,7 @@ def tile_norm_conv_t_kernel(tc, a, conv_kernel, out):
         keep_busy(3)
         fwd(0, 0)
         fwd(0, 1)
-        keep_busy(6)
+        keep_busy(5)
         fwd(1, 0)
         fwd(1, 1)
         evac_with_sums(0, 1)
@@ -418,14 +418,14 @@ def tile_norm_conv_t_kernel(tc, a, conv_kernel, out):
         run(norm(0))
         squares(1, 0)
         back_to_channels(0, "vsvs")
-        keep_busy(2)
+        keep_busy(3)
         fwd(2, 0)
         fwd(2, 1)
-        keep_busy(2)
+        keep_busy(3)
         run(fix_quantise(0))
         squares(1, 1)
         regroup_w(1, 1, "s")
-        run(norm(1))
+        run(norm(1), split_sums(1, 0, 8), 4)
         run(pieces(1, 0, "v", 4))
         quantise_w(1, 0)
         quantise_w(1, 1)
@@ -436,7 +436,7 @@ def tile_norm_conv_t_kernel(tc, a, conv_kernel, out):
             multiply(0, m)
         evac(2, 1)
         back_to_channels(1, "vvvs")
-        run(fix_quantise(1), split_sums(1, 0, 8), 1)
+        run(fix_quantise(1))
         for m in range(4, 7):
             multiply(0, m)
         window_sums(1)
@@ -451,16 +451,17 @@ def tile_norm_conv_t_kernel(tc, a, conv_kernel, out):
             sb = (n + 2) // 2
             new_stats = n % 2 == 0 and sb < NB
             first = 4 if n < 3 else 2
-            r = first + 1
-            for m in range(first):
+            r = first + 3
+            for m in range(first - 1):
                 multiply(n, m)
             math = []
             if new_stats:
                 window_sums(sb)
                 math = math_1(sb)
                 run(math[0:1])
+            multiply(n, first - 1)
             if n + 1 < NCH:
-                back_to_channels(n + 1, "vsvs")
+                back_to_channels(n + 1, "ssvs" if n == 1 else "vsvs")
             for m in range(first, r):
                 multiply(n, m)
             fix = fix_quantise(n + 1) if n + 1 < NCH else []

@@ -335,20 +335,38 @@ def tile_norm_conv_t_kernel(tc, a, conv_kernel, out):
                 scales[b] = gpool.tile([P, 2, 2, 2, 256], U8, name="scales", align_bytes=64)
             r0 = 1 if quad == 0 else 16
             r1 = 16 * quad + 16
-            ops = [lambda: nc.vector.tensor_copy(out=words[:, :, 0, r0:r1, 0], in_=words[:, :, 1, r0:r1, 1])]
+            def edge_column():
+                nc.vector.tensor_copy(out=words[:, :, 0, r0:r1, 0], in_=words[:, :, 1, r0:r1, 1])
+
+            def edge_row(phi, kh):
+                nc.vector.tensor_copy(out=words[:, kh, phi, 0], in_=words[:, 1 - kh, phi, 1])
+
+            def quantise(phi, kh):
+                nc.vector.quantize_mx(
+                    out=codes[b][:, kh, quad, phi, :].bitcast(FP8X4),
+                    scales=scales[b][:, kh, quad, phi, :],
+                    in_=g[:, kh, phi, 1024 * quad : 1024 * quad + 1024],
+                )
+
             if quad == 0:
-                for kh in range(2):
-                    ops.append(lambda kh=kh: nc.vector.tensor_copy(out=words[:, kh, :, 0], in_=words[:, 1 - kh, :, 1]))
-            for phi in (1, 0):
-                for kh in range(2):
-                    ops.append(
-                        lambda phi=phi, kh=kh: nc.vector.quantize_mx(
-                            out=codes[b][:, kh, quad, phi, :].bitcast(FP8X4),
-                            scales=scales[b][:, kh, quad, phi, :],
-                            in_=g[:, kh, phi, 1024 * quad : 1024 * quad + 1024],
-                        )
-                    )
-            return ops
+                return [
+                    lambda: edge_row(1, 0),
+                    lambda: edge_row(1, 1),
+                    edge_column,
+                    lambda: quantise(1, 0),
+                    lambda: edge_row(0, 0),
+                    lambda: edge_row(0, 1),
+                    lambda: quantise(1, 1),
+                    lambda: quantise(0, 0),
+                    lambda: quantise(0, 1),
+                ]
+            return [
+                lambda: quantise(1, 0),
+                edge_column,
+                lambda: quantise(1, 1),
+                lambda: quantise(0, 0),
+                lambda: quantise(0, 1),
+            ]
 
         def multiply(k, m, engine="s"):
             b, quad = k // 2, k % 2
@@ -421,7 +439,7 @@ def tile_norm_conv_t_kernel(tc, a, conv_kernel, out):
         keep_busy(3)
         fwd(2, 0)
         fwd(2, 1)
-        keep_busy(3)
+        keep_busy(1)
         run(fix_quantise(0))
         squares(1, 1)
         regroup_w(1, 1, "s")
@@ -472,9 +490,8 @@ def tile_norm_conv_t_kernel(tc, a, conv_kernel, out):
                 math_root(sb)
             else:
                 run(moments_ops)
-            run(fix, sums)
-            if n + 2 < NCH:
-                run(norm(n + 2))
+            run(fix[:2])
+            run(fix[2:] + (norm(n + 2) if n + 2 < NCH else []), sums)
             if n + 5 < NCH:
                 fwd((n + 5) // 2, (n + 5) % 2)
                 evac((n + 5) // 2, (n + 5) % 2)

from contextlib import ExitStack

import concourse.mybir as mybir
from concourse.masks import make_identity

FLOPS = 2 * 4096 * 1024 * 1024

BF16 = mybir.dt.bfloat16
F32 = mybir.dt.float32
U32 = mybir.dt.uint32
U8 = mybir.dt.uint8
FP8X4 = mybir.dt.float8_e4m3fn_x4
ALU = mybir.AluOpType
ACT = mybir.ActivationFunctionType

P = 128
NB = 4
TPI = 8
NCH = 2 * NB
Z_IN = 130
VARIANTS = [(0, 0), (0, 1), (1, 0), (1, 1)]


def tile_norm_conv_t_kernel(tc, a, conv_kernel, out):
    nc = tc.nc
    with ExitStack() as ctx:
        const = ctx.enter_context(tc.tile_pool(name="const", bufs=1))
        keep = ctx.enter_context(tc.tile_pool(name="keep", bufs=1))
        small = ctx.enter_context(tc.tile_pool(name="small", bufs=2))
        npool = ctx.enter_context(tc.tile_pool(name="npool", bufs=8))
        gpool = ctx.enter_context(tc.tile_pool(name="gpool", bufs=2))
        opool = ctx.enter_context(tc.tile_pool(name="opool", bufs=12))
        ps_w = ctx.enter_context(tc.psum_pool(name="ps_w", bufs=5))
        ps_o = ctx.enter_context(tc.psum_pool(name="ps_o", bufs=3))
        ctx.enter_context(tc.manual_schedule())

        a_sb = []
        for b in range(NB):
            a_b = keep.tile([P, 2, 1024], BF16, name="a_sb%d" % b)
            a_sb.append(a_b)
        w_raw = {}
        for half in range(2):
            for kh in range(2):
                w_part = keep.tile([P, 4, 512], BF16, name="w_raw%d%d" % (half, kh))
                w_raw[(half, kh)] = w_part
        w_view = conv_kernel.rearrange("(q e k w) o -> q e k w o", e=2, k=2, w=2)

        def load_a(b, n=1):
            a_view = a[b].rearrange("(h c) i j -> c h (i j)", h=2)
            for i in range(n):
                pixels = slice(1024 // n * i, 1024 // n * (i + 1))
                nc.sync.dma_start(out=a_sb[b][:, :, pixels], in_=a_view[:, :, pixels])

        def load_w(half):
            cols = slice(512 * half, 512 * half + 512)
            for kh in range(2):
                for e in range(2):
                    nc.sync.dma_start(out=w_raw[(half, kh)][:, e:4:2, :], in_=w_view[:, e, kh, :, cols])

        load_a(0, 2)
        load_w(0)
        load_a(1)
        load_w(1)
        load_a(2)
        load_a(3)

        one = const.tile([P, 1], F32, name="one")
        nc.vector.memset(one[:], 1.0)
        one_rt = const.tile([P, 1], F32, name="one_rt")
        nc.scalar.activation(out=one_rt[:], in_=one[:], func=ACT.Abs_reciprocal_sqrt)

        zeros = const.tile([P, 512], BF16, name="zeros")
        nc.vector.memset(zeros[:], 0.0)
        identb = const.tile([P, P], BF16, name="identb")
        make_identity(nc, identb[:])
        diag = const.tile([P, 388], BF16, name="diag")
        nc.vector.memset(diag[:], 0.0)
        nc.vector.tensor_copy(out=diag[:, Z_IN : Z_IN + P], in_=identb[:])
        pair = const.tile([P, 388], BF16, name="pair")
        nc.vector.tensor_tensor(out=pair[:, 0:387], in0=diag[:, 0:387], in1=diag[:, 1:388], op=ALU.add)
        band = const.tile([P, 356], BF16, name="band")
        nc.vector.tensor_tensor(out=band[:, 0:355], in0=pair[:, 0:355], in1=pair[:, 32:387], op=ALU.add)
        band_odd = const.tile([P, 356], BF16, name="band_odd")
        band_even = const.tile([P, 356], BF16, name="band_even")
        nc.scalar.copy(
            out=band_odd[:, 0:354].rearrange("p (k t) -> p k t", t=2),
            in_=band[:, 0:354].rearrange("p (k t) -> p k t", t=2)[:, :, 0:1].to_broadcast([P, 177, 2]),
        )
        nc.scalar.copy(
            out=band_even[:, 1:355].rearrange("p (k t) -> p k t", t=2),
            in_=band[:, 1:355].rearrange("p (k t) -> p k t", t=2)[:, :, 0:1].to_broadcast([P, 177, 2]),
        )
        nc.scalar.copy(out=band_even[:, 2:354:32], in_=band[:, 2:354:32])
        bands = [band_even, band_odd]
        identf = const.tile([P, P], F32, name="identf")
        make_identity(nc, identf[:])

        wg = keep.tile([P, 2, 1024, 4], BF16, name="wg", align_bytes=64)
        wc = keep.tile([P, 2, 1024], U32, name="wc", align_bytes=64)
        ws = keep.tile([P, 2, 1024], U8, name="ws", align_bytes=64)

        def regroup_w(half, kh, engine, part=slice(0, 512)):
            cols = slice(512 * half + part.start, 512 * half + part.stop)
            dst = wg[:, kh, cols, :].rearrange("q (c i) t -> q c t i", i=4)
            src = w_raw[(half, kh)][:, :, part].rearrange("q t (c i) -> q c t i", i=4)
            if engine == "v":
                nc.vector.tensor_copy(out=dst, in_=src)
            elif engine == "s":
                nc.scalar.copy(out=dst, in_=src)
            else:
                nc.gpsimd.tensor_scalar(out=dst, in0=src, scalar1=1.0, scalar2=0.0, op0=ALU.mult, op1=ALU.add)

        def quantise_w(half, kh):
            cols = slice(512 * half, 512 * half + 512)
            nc.vector.quantize_mx(
                out=wc[:, kh, cols].bitcast(FP8X4),
                scales=ws[:, kh, cols],
                in_=wg[:, kh, cols].rearrange("q o t -> q (o t)"),
            )

        a_t = {}
        parts = {}
        totals = {}
        moments = {}
        front = {}
        wins = {}
        means = {}
        rstds = {}
        devs = {}

        for b in range(NB):
            parts[b] = keep.tile([P, 6, 16], BF16, name="parts%d" % b)
            nc.vector.memset(parts[b][:], 0.0)

        def keep_busy(n):
            idle = ps_w.tile([P, 512], F32, name="idle", tag="work")
            for i in range(n):
                nc.tensor.matmul(out=idle[:], lhsT=zeros[:, 0:P], rhs=zeros[:], start=True, stop=True)

        def fwd(b, quad):
            if quad == 0:
                a_t[b] = keep.tile([P, TPI, 256], BF16, name="a_t%d" % b)
                moments[b] = keep.tile([P, TPI, 6], F32, name="moments%d" % b)
                totals[b] = keep.tile([P, 2, TPI], F32, name="totals%d" % b)
            f_t = ps_w.tile([P, 4, 256], BF16, name="f_t", tag="work")
            front[(b, quad)] = f_t
            for tl in range(4):
                t = 4 * quad + tl
                for h in range(2):
                    nc.tensor.transpose(
                        out=f_t[:, tl, P * h : P * h + P],
                        in_=a_sb[b][:, h, P * t : P * t + P],
                        identity=identb[:],
                    )

        def evac(b, quad):
            nc.scalar.copy(out=a_t[b][:, 4 * quad : 4 * quad + 4, :], in_=front[(b, quad)][:])

        def evac_with_sums(b, quad):
            for tl in range(4):
                t = 4 * quad + tl
                nc.scalar.activation(
                    out=a_t[b][:, t, :],
                    in_=front[(b, quad)][:, tl, :],
                    func=ACT.Copy,
                    accum_out=totals[b][:, 0, t : t + 1],
                )

        def squares(b, quad):
            for t in range(4 * quad, 4 * quad + 4):
                junk = small.tile([P, 256], BF16, name="junk")
                nc.scalar.activation(
                    out=junk[:], in_=a_t[b][:, t, :], func=ACT.Square, accum_out=totals[b][:, 1, t : t + 1]
                )

        def pixel_moments(b, quad, from_bank=False):
            return [
                lambda tl=tl: nc.vector.bn_stats(
                    out=moments[b][:, 4 * quad + tl, :],
                    in_=front[(b, quad)][:, tl, :] if from_bank else a_t[b][:, 4 * quad + tl, :],
                )
                for tl in range(4)
            ]

        def pixel_sums(b, t0, t1):
            n = t1 - t0
            total = totals[b]
            mom = moments[b][:, t0:t1, :].rearrange("p t (e s) -> p t e s", e=2)
            mean, m2 = mom[:, :, :, 1], mom[:, :, :, 2]
            half = small.tile([P, n, 2], F32, name="half_%d" % n)
            sq2 = small.tile([P, n, 2], F32, name="sq2_%d" % n)
            q2 = small.tile([P, n, 2], F32, name="q2_%d" % n)
            return [
                lambda: nc.vector.tensor_scalar(out=half[:], in0=mean, scalar1=128.0, scalar2=None, op0=ALU.mult),
                lambda: nc.vector.scalar_tensor_tensor(
                    out=sq2[:], in0=mean, scalar=128.0, in1=mean, op0=ALU.mult, op1=ALU.mult
                ),
                lambda: nc.vector.tensor_tensor(
                    out=total[:, 0, t0:t1], in0=half[:, :, 0], in1=half[:, :, 1], op=ALU.add
                ),
                lambda: nc.vector.tensor_tensor(out=q2[:], in0=sq2[:], in1=m2, op=ALU.add),
                lambda: nc.vector.tensor_tensor(
                    out=total[:, 1, t0:t1], in0=q2[:, :, 0], in1=q2[:, :, 1], op=ALU.add
                ),
            ]

        def split_sums(b, t0, t1):
            total = totals[b][:, :, t0:t1]
            rest_t = small.tile([P, 2, t1 - t0], F32, name="rest_%d" % (t1 - t0))
            rest = rest_t[:]
            hi, mid, lo = [parts[b][:, 2 * a : 2 * a + 2, 1 + t0 : 1 + t1] for a in range(3)]
            return [
                lambda: nc.vector.tensor_copy(out=hi, in_=total),
                lambda: nc.vector.tensor_tensor(out=rest, in0=total, in1=hi, op=ALU.subtract),
                lambda: nc.vector.tensor_copy(out=mid, in_=rest),
                lambda: nc.vector.tensor_tensor(out=lo, in0=rest, in1=mid, op=ALU.subtract),
            ]

        def window_sums(b):
            win = ps_w.tile([P, 4, 48], F32, name="win", tag="work")
            wins[b] = win
            for v, (kh, phi) in enumerate(VARIANTS):
                side = 1 if kh == 0 else -1
                z0 = Z_IN - 32 * kh
                dst = win[:, v].rearrange("p (x t) -> p x t", t=TPI)
                nc.tensor.matmul(
                    out=dst,
                    lhsT=bands[phi][:, z0 : z0 + P],
                    rhs=parts[b][:, :, 1 : 1 + TPI],
                    start=True,
                    stop=False,
                )
                z1 = z0 - P * side
                nc.tensor.matmul(
                    out=dst,
                    lhsT=bands[phi][:, z1 : z1 + P],
                    rhs=parts[b][:, :, 1 + side : 1 + side + TPI],
                    start=False,
                    stop=True,
                )

        def math_1(b):
            wsum = small.tile([P, 4, 16], F32, name="wsum")
            means[b] = keep.tile([P, 4, TPI], F32, name="mean%d" % b)
            sq = small.tile([P, 4, TPI], F32, name="sq")
            devs[b] = small.tile([P, 4, TPI], F32, name="dev")
            return [
                lambda: nc.vector.tensor_reduce(
                    out=wsum[:],
                    in_=wins[b][:].rearrange("p v (a x) -> p v x a", a=3),
                    axis=mybir.AxisListType.X,
                    op=ALU.add,
                ),
                lambda: nc.vector.scalar_tensor_tensor(
                    out=sq[:],
                    in0=wsum[:, :, 0:TPI],
                    scalar=1.0 / 1024.0,
                    in1=wsum[:, :, 0:TPI],
                    op0=ALU.mult,
                    op1=ALU.mult,
                ),
                lambda: nc.vector.tensor_scalar(
                    out=means[b][:], in0=wsum[:, :, 0:TPI], scalar1=1.0 / 1024.0, scalar2=None, op0=ALU.mult
                ),
                lambda: nc.vector.tensor_tensor(
                    out=devs[b][:], in0=wsum[:, :, TPI:16], in1=sq[:], op=ALU.subtract
                ),
            ]

        def math_root(b):
            rstds[b] = keep.tile([P, 4, TPI], F32, name="rstd%d" % b)
            nc.scalar.activation(out=rstds[b][:], in_=devs[b][:], func=ACT.Abs_reciprocal_sqrt, scale=1.0 / 1023.0)

        grouped = {}
        codes = {}
        scales = {}
        normed = {}
        back = {}

        def norm(k):
            b, quad = k // 2, k % 2
            ops = []
            for v in range(4):
                n_q = npool.tile([P, 4, 256], BF16, name="n_q")
                normed[(k, v)] = n_q
                for tl in range(4):
                    t = 4 * quad + tl
                    ops.append(
                        lambda v=v, tl=tl, t=t, n_q=n_q: nc.vector.tensor_scalar(
                            out=n_q[:, tl, :],
                            in0=a_t[b][:, t, :],
                            scalar1=means[b][:, v, t : t + 1],
                            scalar2=rstds[b][:, v, t : t + 1],
                            op0=ALU.subtract,
                            op1=ALU.mult,
                        )
                    )
            return ops

        def bwd(k, v):
            bk = ps_w.tile([P, 512], F32, name="bk", tag="work")
            back[(k, v)] = bk
            for tl in range(4):
                nc.tensor.transpose(
                    out=bk[:, P * tl : P * tl + P],
                    in_=normed[(k, v)][:, tl, :].bitcast(F32),
                    identity=identf[:],
                )

        def copy_out(k, v, engine):
            b, quad = k // 2, k % 2
            kh, phi = VARIANTS[v]
            if quad == 0 and v == 0:
                grouped[b] = gpool.tile([P, 2, 2, 2048], BF16, name="grouped", align_bytes=64)
            lo = 1 if (kh == 1 and quad == 0) else 0
            hi = 15 if (kh == 0 and quad == 1) else 16
            d0 = 32 * (16 * quad + lo + 1 - kh)
            n = 32 * (hi - lo)
            s = 1 - phi
            dst = grouped[b][:, kh, phi, :].bitcast(F32)[:, d0 + s : d0 + n]
            src = back[(k, v)][:, 32 * lo : 32 * hi - s]
            if engine == "v":
                nc.vector.tensor_copy(out=dst, in_=src)
            else:
                nc.scalar.copy(out=dst, in_=src)

        def fix_quantise(k):
            b, quad = k // 2, k % 2
            g = grouped[b]
            words = g[:].rearrange("p h f x -> p (h f x)").bitcast(F32).rearrange(
                "p (h f r x) -> p h f r x", h=2, f=2, r=32
            )
            if quad == 0:
                codes[b] = gpool.tile([P, 2, 2, 2, 256], U32, name="codes", align_bytes=64)
                scales[b] = gpool.tile([P, 2, 2, 2, 256], U8, name="scales", align_bytes=64)
            r0 = 1 if quad == 0 else 16
            r1 = 16 * quad + 16
            def edge_column():
                nc.vector.tensor_copy(out=words[:, :, 0, r0:r1, 0], in_=words[:, :, 1, r0:r1, 1])

            def edge_row(phi, kh):
                nc.vector.tensor_copy(out=words[:, kh, phi, 0], in_=words[:, 1 - kh, phi, 1])

            def quantise(phi, kh):
                nc.vector.quantize_mx(
                    out=codes[b][:, kh, quad, phi, :].bitcast(FP8X4),
                    scales=scales[b][:, kh, quad, phi, :],
                    in_=g[:, kh, phi, 1024 * quad : 1024 * quad + 1024],
                )

            if quad == 0:
                return [
                    lambda: edge_row(1, 0),
                    lambda: edge_row(1, 1),
                    edge_column,
                    lambda: quantise(1, 0),
                    lambda: edge_row(0, 0),
                    lambda: edge_row(0, 1),
                    lambda: quantise(1, 1),
                    lambda: quantise(0, 0),
                    lambda: quantise(0, 1),
                ]
            return [
                lambda: quantise(1, 0),
                edge_column,
                lambda: quantise(1, 1),
                lambda: quantise(0, 0),
                lambda: quantise(0, 1),
            ]

        def multiply(k, m, engine="s"):
            b, quad = k // 2, k % 2
            acc = ps_o.tile([P, 512], F32, name="acc")
            for kh in range(2):
                nc.tensor.matmul_mx(
                    out=acc[:],
                    lhsT=wc[:, kh, P * m : P * m + P].bitcast(FP8X4),
                    lhsT_scale=ws[:, kh, P * m : P * m + P],
                    rhs=codes[b][:, kh, quad].rearrange("p f x -> p (f x)").bitcast(FP8X4),
                    rhs_scale=scales[b][:, kh, quad].rearrange("p f x -> p (f x)"),
                    start=(kh == 0),
                    stop=(kh == 1),
                )
            o_sb = opool.tile([P, 512], F32, name="o_sb")
            dst, src = o_sb[:].rearrange("p (x f) -> p x f", f=2), acc[:].rearrange("p (f x) -> p x f", f=2)
            if engine == "v":
                nc.vector.tensor_copy(out=dst, in_=src)
            else:
                nc.scalar.copy(out=dst, in_=src)
            nc.sync.dma_start(
                out=out[b, P * m : P * m + P, 16 * quad : 16 * quad + 16, :].rearrange("o i j -> o (i j)"),
                in_=o_sb[:],
            )

        def back_to_channels(k, engines="vsvs"):
            for v in range(4):
                bwd(k, v)
                copy_out(k, v, engines[v])

        def run(ops, between=(), every=1):
            done = 0
            for i, op in enumerate(ops):
                op()
                if i % every == every - 1 and done < len(between):
                    between[done]()
                    done += 1
            for op in between[done:]:
                op()

        def pieces(half, kh, engine, n):
            return [
                lambda i=i: regroup_w(half, kh, engine, slice(512 // n * i, 512 // n * (i + 1))) for i in range(n)
            ]

        keep_busy(3)
        fwd(0, 0)
        fwd(0, 1)
        keep_busy(5)
        fwd(1, 0)
        fwd(1, 1)
        evac_with_sums(0, 1)
        run(pixel_moments(0, 0, True))
        squares(0, 1)
        evac(0, 0)
        fill = pieces(0, 0, "v", 4) + pieces(0, 1, "v", 4)
        run(pixel_sums(0, 0, 4), fill[0:4])
        run(split_sums(0, 0, 8), fill[4:8])
        window_sums(0)
        keep_busy(4)
        evac_with_sums(1, 0)
        evac_with_sums(1, 1)
        quantise_w(0, 0)
        run(math_1(0))
        math_root(0)
        quantise_w(0, 1)
        run(norm(0))
        squares(1, 0)
        back_to_channels(0, "vsvs")
        keep_busy(3)
        fwd(2, 0)
        fwd(2, 1)
        keep_busy(1)
        run(fix_quantise(0))
        squares(1, 1)
        regroup_w(1, 1, "s")
        run(norm(1), split_sums(1, 0, 8), 4)
        run(pieces(1, 0, "v", 4))
        quantise_w(1, 0)
        quantise_w(1, 1)
        for m in range(2):
            multiply(0, m)
        evac(2, 0)
        for m in range(2, 4):
            multiply(0, m)
        evac(2, 1)
        back_to_channels(1, "vvvs")
        run(fix_quantise(1))
        for m in range(4, 7):
            multiply(0, m)
        window_sums(1)
        for m in range(7, 8):
            multiply(0, m)
        run(math_1(1))
        math_root(1)
        run(pixel_moments(2, 0))
        run(norm(2))
        for n in range(1, NCH):
            fb, fq = (n + 4) // 2, (n + 4) % 2
            sb = (n + 2) // 2
            new_stats = n % 2 == 0 and sb < NB
            first = 4 if n < 3 else 2
            r = first + 3
            for m in range(first - 1):
                multiply(n, m)
            math = []
            if new_stats:
                window_sums(sb)
                math = math_1(sb)
                run(math[0:1])
            multiply(n, first - 1)
            if n + 1 < NCH:
                back_to_channels(n + 1, "ssvs" if n == 1 else "vsvs")
            for m in range(first, r):
                multiply(n, m)
            fix = fix_quantise(n + 1) if n + 1 < NCH else []
            moments_ops = pixel_moments(fb, fq) if fb < NB else []
            sums = pixel_sums(fb, 0, 8) + split_sums(fb, 0, 8) if fb < NB and fq == 1 else []
            if new_stats:
                run(moments_ops, math[1:])
                math_root(sb)
            else:
                run(moments_ops)
            run(fix[:2])
            run(fix[2:] + (norm(n + 2) if n + 2 < NCH else []), sums)
            if n + 5 < NCH:
                fwd((n + 5) // 2, (n + 5) % 2)
                evac((n + 5) // 2, (n + 5) % 2)
            for m in range(r, 8):
                multiply(n, m)
